import numpy as np
import ml_dtypes


def mxq(x, axis, fmt="e4m3"):
    dtype, down = {"e4m3": (ml_dtypes.float8_e4m3fn, 7), "e5m2": (ml_dtypes.float8_e5m2, 14)}[fmt]
    v = np.moveaxis(np.asarray(x, np.float32).astype(ml_dtypes.bfloat16).astype(np.float64), axis, -1)
    blocks = v.reshape(v.shape[:-1] + (-1, 32))
    amax = np.abs(blocks).max(-1, keepdims=True)
    byte = np.maximum(np.where(amax > 0, np.frexp(amax)[1] - 1 + 127, 0) - down, 1)
    scale = np.exp2(byte - 127.0)
    codes = (blocks / scale).astype(np.float32).astype(dtype).astype(np.float64)
    return np.moveaxis((codes * scale).reshape(v.shape), -1, axis)


WIDE = False


def mx_kscale(k):
    if not WIDE:
        return np.ones(k)
    levels = np.array([10, -10, 5, -5, 0])
    a = np.random.permutation(np.resize(levels, k // 512 * 4)).reshape(k // 512, 4)
    idx = np.arange(k)
    return np.exp2(a[idx // 512, idx % 128 // 32])


BF16 = ml_dtypes.bfloat16


def bf(x):
    return np.asarray(x, np.float32).astype(BF16)


def f64(x):
    return np.asarray(x).astype(np.float64)


E2M1 = np.array([0.0, 0.5, 1.0, 1.5, 2.0, 3.0, 4.0, 6.0, -0.0, -0.5, -1.0, -1.5, -2.0, -3.0, -4.0, -6.0])


def pack_weight(w, fmt):
    k, n = w.shape
    w = f64(bf(w)).reshape(k // 32, 32, n)
    amax = np.abs(w).max(1)
    if fmt == "e4m3":
        byte = np.frexp(amax)[1] - 1 + 127 - 7
    else:
        mant, ex = np.frexp(amax / 6.0)
        byte = np.where(mant > 0.5, ex, ex - 1) + 127
    byte = np.clip(np.where(amax > 0, byte, 1), 1, 254)
    scaled = (w * np.exp2(127.0 - byte)[:, None, :]).reshape(k, n).astype(np.float32)
    by_word = np.ascontiguousarray(scaled.reshape(k // 512, 128, 4, n).transpose(0, 1, 3, 2))
    if fmt == "e4m3":
        words = by_word.astype(ml_dtypes.float8_e4m3fn).view(np.uint8)
    else:
        c = by_word.astype(ml_dtypes.float4_e2m1fn).view(np.uint8) & 0xF
        words = c[..., 0::2] | (c[..., 1::2] << 4)
    return np.ascontiguousarray(words), np.ascontiguousarray(byte.astype(np.uint8).reshape(k // 512, 16, n))


def unpack_weight(words, scales, fmt):
    g, p, n, _ = words.shape
    if fmt == "e4m3":
        vals = np.ascontiguousarray(words).view(ml_dtypes.float8_e4m3fn).astype(np.float64)
    else:
        nib = np.empty((g, p, n, 4), np.uint8)
        nib[..., 0::2] = words & 0xF
        nib[..., 1::2] = words >> 4
        vals = E2M1[nib]
    vals = vals * np.repeat(np.exp2(scales.astype(np.float64) - 127.0), 8, axis=1)[..., None]
    return vals.transpose(0, 1, 3, 2).reshape(g * 512, n)


N, F, U, G, P = 4096, 512, 256, 3, 3
C = G + P
T = G + 2 * P + 1
LO, HI = -1.0, 1.0
LN_EPS = 0.001
FMT = "e4m3"


def b_splines(x, grid):
    xe = x[..., None]
    bases = np.where((xe >= grid[..., :-1]) & (xe < grid[..., 1:]), 1.0, 0.0)
    for k in range(1, P + 1):
        left = (xe - grid[..., :-(k + 1)]) / (grid[..., k:-1] - grid[..., :-(k + 1)])
        right = (grid[..., k + 1:] - xe) / (grid[..., k + 1:] - grid[..., 1:-k])
        bases = left * bases[..., :-1] + right * bases[..., 1:]
    return bases.reshape(x.shape[0], -1)


def setup_inputs():
    t = mx_kscale(F)
    h = (HI - LO) / G
    knots = np.linspace(LO - P * h, LO + (G + P) * h, T)
    grid = knots[None, None, :] + (np.random.random_sample((1, F, T)) - 0.5) * 0.25 * h
    x = bf(np.random.standard_normal((N, F)) * 0.1 + np.random.standard_normal((N, 1)) * 0.1)
    ln_gamma = bf((1.0 + 0.1 * np.random.standard_normal(F)) * t)
    ln_beta = bf(0.1 * np.random.standard_normal(F) * t)
    base_weight_words, base_weight_scales = pack_weight(np.random.standard_normal((F, U)) / np.sqrt(F) / t[:, None], FMT)
    base_bias = bf(0.25 * np.random.standard_normal(U))
    spline_weight_words, spline_weight_scales = pack_weight(np.random.standard_normal((F * C, U)) / np.sqrt(F), FMT)
    return {
        "x": x,
        "ln_gamma": ln_gamma,
        "ln_beta": ln_beta,
        "base_weight_words": base_weight_words,
        "base_weight_scales": base_weight_scales,
        "base_bias": base_bias,
        "spline_weight_words": spline_weight_words,
        "spline_weight_scales": spline_weight_scales,
        "grid": bf(grid * t[None, :, None]),
    }


def reference(x, ln_gamma, ln_beta, base_weight_words, base_weight_scales, base_bias, spline_weight_words, spline_weight_scales, grid):
    x = f64(x)
    mean = x.mean(-1, keepdims=True)
    var = x.var(-1, keepdims=True)
    xn = (x - mean) / np.sqrt(var + LN_EPS) * f64(ln_gamma) + f64(ln_beta)
    base_out = (mxq(np.maximum(xn, 0.0), 1, "e4m3") @ unpack_weight(base_weight_words, base_weight_scales, FMT)) + f64(base_bias)
    spline_out = mxq(b_splines(xn, f64(grid)), 1, "e4m3") @ unpack_weight(spline_weight_words, spline_weight_scales, FMT)
    return base_out + spline_out

@@ -1,0 +1,335 @@
+from contextlib import ExitStack
+
+import concourse.masks as masks
+import concourse.mybir as mybir
+
+F32 = mybir.dt.float32
+BF16 = mybir.dt.bfloat16
+I32 = mybir.dt.int32
+U32 = mybir.dt.uint32
+U8 = mybir.dt.uint8
+FP8X4 = mybir.dt.float8_e4m3fn_x4
+ALU = mybir.AluOpType
+FUNC = mybir.ActivationFunctionType
+
+ROWS = 4096
+FEATURES = 512
+UNITS = 256
+KNOTS = 10
+BASES = 6
+LN_EPS = 0.001
+
+P = 128
+PACK = 4
+SLOTS = FEATURES // P
+WORDS = SLOTS * BASES // PACK
+SHARES = 6
+BLOCK_PARTITIONS = 8
+CHUNK = 512
+ROW_TILES = CHUNK // P
+CHUNKS = ROWS // CHUNK
+
+FLOPS = 2 * ROWS * (FEATURES + FEATURES * BASES) * UNITS
+
+
+def product(nc, pool, name, factors):
+    result = pool.tile([P, SLOTS, BASES], F32, name=name)
+    nc.vector.tensor_mul(out=result[:], in0=factors[0], in1=factors[1])
+    for factor in factors[2:]:
+        nc.vector.tensor_mul(out=result[:], in0=result[:], in1=factor)
+    return result
+
+
+def tile_kanlinear_pa_t_kernel(
+    tc,
+    x,
+    ln_gamma,
+    ln_beta,
+    base_weight_words,
+    base_weight_scales,
+    base_bias,
+    spline_weight_words,
+    spline_weight_scales,
+    grid,
+    out,
+):
+    nc = tc.nc
+    with ExitStack() as stack:
+        keep = stack.enter_context(tc.tile_pool(name="keep", bufs=1))
+        rows_pool = stack.enter_context(tc.tile_pool(name="rows", bufs=2))
+        small = stack.enter_context(tc.tile_pool(name="small", bufs=2))
+        xn_pool = stack.enter_context(tc.tile_pool(name="xn", bufs=2))
+        work = stack.enter_context(tc.tile_pool(name="work", bufs=3))
+        plane_pool = stack.enter_context(tc.tile_pool(name="planes", bufs=2))
+        operand_pool = stack.enter_context(tc.tile_pool(name="operands", bufs=3))
+        result_pool = stack.enter_context(tc.tile_pool(name="results", bufs=4))
+        transposed_pool = stack.enter_context(tc.psum_pool(name="transposed", bufs=4))
+        acc_pool = stack.enter_context(tc.psum_pool(name="acc", bufs=ROW_TILES))
+
+        def normalised_chunk(c):
+            x_rows = rows_pool.tile([P, ROW_TILES, FEATURES], BF16)
+            nc.sync.dma_start(
+                out=x_rows[:],
+                in_=x[c * CHUNK : (c + 1) * CHUNK, :].rearrange("(t p) f -> p t f", p=P),
+            )
+            stats = small.tile([P, ROW_TILES, 6], F32)
+            mean_var = small.tile([P, ROW_TILES, 2], F32)
+            for t in range(ROW_TILES):
+                nc.vector.bn_stats(out=stats[:, t, :], in_=x_rows[:, t, :])
+                nc.vector.bn_aggr(out=mean_var[:, t, :], in_=stats[:, t, :])
+            var_eps = small.tile([P, ROW_TILES], F32)
+            nc.vector.tensor_scalar_add(out=var_eps[:], in0=mean_var[:, :, 1], scalar1=LN_EPS)
+            std = small.tile([P, ROW_TILES], F32)
+            nc.scalar.activation(out=std[:], in_=var_eps[:], func=FUNC.Sqrt)
+            rough = small.tile([P, ROW_TILES], F32)
+            nc.vector.reciprocal(out=rough[:], in_=std[:])
+            step = small.tile([P, ROW_TILES], F32)
+            nc.vector.tensor_mul(out=step[:], in0=rough[:], in1=rough[:])
+            nc.vector.tensor_mul(out=step[:], in0=step[:], in1=var_eps[:])
+            nc.vector.tensor_scalar(
+                out=step[:], in0=step[:], scalar1=-0.5, scalar2=1.5, op0=ALU.mult, op1=ALU.add
+            )
+            rstd = small.tile([P, ROW_TILES], F32)
+            nc.vector.tensor_mul(out=rstd[:], in0=rough[:], in1=step[:])
+            z = rows_pool.tile([P, ROW_TILES, SLOTS, P], F32)
+            for t in range(ROW_TILES):
+                nc.vector.tensor_scalar(
+                    out=z[:, t, :, :],
+                    in0=x_rows[:, t, :].rearrange("p (q s) -> p s q", s=SLOTS),
+                    scalar1=mean_var[:, t, 0:1],
+                    scalar2=rstd[:, t : t + 1],
+                    op0=ALU.subtract,
+                    op1=ALU.mult,
+                )
+            xn = xn_pool.tile([P, SLOTS, CHUNK], F32)
+            for s in range(SLOTS):
+                z_t = transposed_pool.tile([P, CHUNK], F32)
+                for t in range(ROW_TILES):
+                    nc.tensor.transpose(z_t[:, t * P : (t + 1) * P], z[:, t, s, :], identity[:])
+                nc.scalar.activation(
+                    out=xn[:, s, :],
+                    in_=z_t[:],
+                    func=FUNC.Identity,
+                    scale=gamma[:, s : s + 1],
+                    bias=beta[:, s : s + 1],
+                )
+            return xn
+
+        def quantise_relu(planes):
+            grouped = operand_pool.tile([P, CHUNK, PACK], BF16, align_bytes=64)
+            nc.scalar.activation(
+                out=grouped[:], in_=planes.rearrange("p t r -> p r t"), func=FUNC.Relu
+            )
+            codes = operand_pool.tile([P, CHUNK], U32, align_bytes=64)
+            scales = operand_pool.tile([P, CHUNK], U8, align_bytes=64)
+            nc.vector.quantize_mx(
+                out=codes[:].bitcast(FP8X4),
+                scales=scales[:],
+                in_=grouped[:].rearrange("p r t -> p (r t)"),
+            )
+            return codes, scales
+
+        def multiply(acc, operand, weight_words, weight_scales, start, stop):
+            codes, scales = operand
+            for t in range(ROW_TILES):
+                nc.tensor.matmul_mx(
+                    out=acc[t][:],
+                    lhsT=codes[:, t * P : (t + 1) * P].bitcast(FP8X4),
+                    lhsT_scale=scales[:, t * P : (t + 1) * P],
+                    rhs=weight_words.bitcast(FP8X4),
+                    rhs_scale=weight_scales,
+                    start=start,
+                    stop=stop,
+                )
+
+        identity = keep.tile([P, P], F32)
+        masks.make_identity(nc, identity[:])
+        gamma_bf = keep.tile([P, SLOTS], BF16)
+        beta_bf = keep.tile([P, SLOTS], BF16)
+        knot_bf = keep.tile([P, SLOTS, KNOTS], BF16)
+        nc.sync.dma_start(out=gamma_bf[:], in_=ln_gamma.rearrange("(p s) -> p s", s=SLOTS))
+        nc.sync.dma_start(out=beta_bf[:], in_=ln_beta.rearrange("(p s) -> p s", s=SLOTS))
+        nc.sync.dma_start(out=knot_bf[:], in_=grid.rearrange("o (p s) k -> (o p) s k", s=SLOTS))
+        gamma = keep.tile([P, SLOTS], F32)
+        beta = keep.tile([P, SLOTS], F32)
+        nc.vector.tensor_copy(out=gamma[:], in_=gamma_bf[:])
+        nc.vector.tensor_copy(out=beta[:], in_=beta_bf[:])
+        xn_next = normalised_chunk(0)
+
+        knot = keep.tile([P, SLOTS, KNOTS], F32)
+        nc.vector.tensor_copy(out=knot[:], in_=knot_bf[:])
+        neg_knot = keep.tile([P, SLOTS, KNOTS], F32)
+        nc.vector.tensor_scalar_mul(out=neg_knot[:], in0=knot[:], scalar1=-1.0)
+        span = {}
+        for d in range(1, 5):
+            span[d] = keep.tile([P, SLOTS, KNOTS - d], F32, name="span%d" % d)
+            nc.vector.tensor_sub(
+                out=span[d][:], in0=knot[:, :, d:KNOTS], in1=knot[:, :, 0 : KNOTS - d]
+            )
+
+        def spans(d, first):
+            return span[d][:, :, first : first + BASES]
+
+        c0 = product(nc, keep, "c0", [spans(1, 0), spans(2, 0), spans(3, 0)])
+        nc.vector.reciprocal(out=c0[:], in_=c0[:])
+        c1 = product(nc, keep, "c1", [spans(1, 0), spans(1, 1), spans(2, 1), spans(3, 1)])
+        nc.vector.reciprocal(out=c1[:], in_=c1[:])
+        nc.vector.tensor_mul(out=c1[:], in0=c1[:], in1=spans(4, 0))
+        neg_c4 = product(nc, keep, "neg_c4", [spans(3, 1), spans(2, 2), spans(1, 3)])
+        nc.vector.reciprocal(out=neg_c4[:], in_=neg_c4[:])
+        nc.vector.tensor_scalar_mul(out=neg_c4[:], in0=neg_c4[:], scalar1=-1.0)
+        neg_c3 = product(nc, keep, "neg_c3", [spans(3, 0), spans(2, 1), spans(1, 2), spans(1, 3)])
+        nc.vector.reciprocal(out=neg_c3[:], in_=neg_c3[:])
+        nc.vector.scalar_tensor_tensor(
+            out=neg_c3[:], in0=neg_c3[:], scalar=-1.0, in1=spans(4, 0), op0=ALU.mult, op1=ALU.mult
+        )
+
+        bias_bf = keep.tile([P, UNITS], BF16)
+        nc.sync.dma_start(out=bias_bf[:], in_=base_bias.partition_broadcast(P))
+        bias = keep.tile([P, UNITS], F32)
+        nc.vector.tensor_copy(out=bias[:], in_=bias_bf[:])
+
+        weight_scales = keep.tile([P, SHARES + 1, UNITS], U8, align_bytes=64)
+        nc.vector.memset(weight_scales[:].bitcast(I32), 0)
+        spline_scale_rows = (
+            spline_weight_scales.rearrange("g r n -> (g r) n")
+            .bitcast(I32)
+            .rearrange("(a b c) n -> b a c n", a=4, b=4, c=SHARES)
+        )
+        base_scale_rows = (
+            base_weight_scales.rearrange("g r n -> (g r) n")
+            .bitcast(I32)
+            .rearrange("(a b) n -> b a n", a=4)
+        )
+        for b in range(4):
+            nc.sync.dma_start(
+                out=weight_scales[b:P:32, 0:SHARES, :].bitcast(I32), in_=spline_scale_rows[b]
+            )
+            nc.sync.dma_start(
+                out=weight_scales[b:P:32, SHARES, :].bitcast(I32), in_=base_scale_rows[b]
+            )
+        base_words = keep.tile([P, UNITS], I32, align_bytes=64)
+        nc.sync.dma_start(
+            out=base_words[:],
+            in_=base_weight_words.rearrange("g p n t -> (g p) (n t)").bitcast(I32),
+        )
+        spline_words = keep.tile([P, WORDS, SHARES, UNITS], I32, align_bytes=64)
+        nc.vector.memset(spline_words[:], 0)
+        word_rows = (
+            spline_weight_words.rearrange("g p n t -> (g p) (n t)")
+            .bitcast(I32)
+            .rearrange("(q i e) n -> i q e n", i=BLOCK_PARTITIONS, e=WORDS)
+        )
+        for i in range(BLOCK_PARTITIONS):
+            for c in range(SHARES):
+                members = [e for e in range(WORDS) if (WORDS * i + e) // BLOCK_PARTITIONS == c]
+                if members:
+                    first, last = members[0], members[-1] + 1
+                    nc.sync.dma_start(
+                        out=spline_words[i:P:BLOCK_PARTITIONS, first:last, c, :],
+                        in_=word_rows[i][:, first:last, :],
+                    )
+
+        for chunk in range(CHUNKS):
+            xn = xn_next
+            if chunk + 1 < CHUNKS:
+                xn_next = normalised_chunk(chunk + 1)
+
+            acc = [
+                acc_pool.tile([P, UNITS], F32, name="acc%d" % t, tag="acc") for t in range(ROW_TILES)
+            ]
+            multiply(
+                acc,
+                quantise_relu(xn[:]),
+                base_words[:],
+                weight_scales[:, SHARES, :],
+                start=True,
+                stop=False,
+            )
+
+            planes = plane_pool.tile([P, SLOTS * BASES, CHUNK], BF16)
+            words_done = 0
+            for s in range(SLOTS):
+                v = xn[:, s, :]
+                cube = {}
+                fall_inner = {}
+                rise = {}
+                for i in range(KNOTS):
+                    square = work.tile([P, CHUNK], F32)
+                    nc.scalar.activation(
+                        out=square[:],
+                        in_=v,
+                        func=FUNC.Square,
+                        bias=neg_knot[:, s, i : i + 1],
+                        scale=1.0,
+                    )
+                    cube[i] = work.tile([P, CHUNK], F32, name="cube", tag="cube", bufs=4)
+                    nc.vector.scalar_tensor_tensor(
+                        out=cube[i][:],
+                        in0=v,
+                        scalar=knot[:, s, i : i + 1],
+                        in1=square[:],
+                        op0=ALU.subtract,
+                        op1=ALU.mult,
+                    )
+                    if 1 <= i <= BASES:
+                        j = i - 1
+                        rise_inner = work.tile([P, CHUNK], F32)
+                        nc.scalar.activation(
+                            out=rise_inner[:],
+                            in_=cube[i][:],
+                            func=FUNC.Relu,
+                            scale=c1[:, s, j : j + 1],
+                        )
+                        rise[j] = work.tile([P, CHUNK], BF16, name="rise", tag="rise", bufs=6)
+                        nc.vector.scalar_tensor_tensor(
+                            out=rise[j][:],
+                            in0=cube[j][:],
+                            scalar=c0[:, s, j : j + 1],
+                            in1=rise_inner[:],
+                            op0=ALU.mult,
+                            op1=ALU.subtract,
+                        )
+                    if 3 <= i < 3 + BASES:
+                        fall_inner[i] = work.tile(
+                            [P, CHUNK], F32, name="fall_inner", tag="fall_inner", bufs=4
+                        )
+                        nc.scalar.activation(
+                            out=fall_inner[i][:],
+                            in_=cube[i][:],
+                            func=FUNC.Relu,
+                            scale=neg_c3[:, s, i - 3 : i - 2],
+                        )
+                    if i >= 4:
+                        j = i - 4
+                        fall = work.tile([P, CHUNK], BF16)
+                        nc.vector.scalar_tensor_tensor(
+                            out=fall[:],
+                            in0=cube[i][:],
+                            scalar=neg_c4[:, s, j : j + 1],
+                            in1=fall_inner[i - 1][:],
+                            op0=ALU.mult,
+                            op1=ALU.subtract,
+                        )
+                        nc.vector.tensor_max(
+                            out=planes[:, BASES * s + j, :], in0=rise[j][:], in1=fall[:]
+                        )
+                words_ready = BASES * (s + 1) // PACK
+                for e in range(words_done, words_ready):
+                    operand = quantise_relu(planes[:, PACK * e : PACK * (e + 1), :])
+                    for c in range(SHARES):
+                        multiply(
+                            acc,
+                            operand,
+                            spline_words[:, e, c, :],
+                            weight_scales[:, c, :],
+                            start=False,
+                            stop=(e == WORDS - 1 and c == SHARES - 1),
+                        )
+                words_done = words_ready
+
+            for t in range(ROW_TILES):
+                result = result_pool.tile([P, UNITS], F32)
+                nc.vector.tensor_add(out=result[:], in0=acc[t][:], in1=bias[:])
+                first_row = chunk * CHUNK + t * P
+                nc.sync.dma_start(out=out[first_row : first_row + P, :], in_=result[:])

@@ -28,6 +28,9 @@ BLOCK_PARTITIONS = 8
 CHUNK = 512
 ROW_TILES = CHUNK // P
 CHUNKS = ROWS // CHUNK
+ROUNDS = CHUNKS * SLOTS
+RUN = 4
+VECTOR_WORD = 3
 
 FLOPS = 2 * ROWS * (FEATURES + FEATURES * BASES) * UNITS
 
@@ -59,67 +62,93 @@ def tile_kanlinear_pa_t_kernel(
         rows_pool = stack.enter_context(tc.tile_pool(name="rows", bufs=2))
         small = stack.enter_context(tc.tile_pool(name="small", bufs=2))
         xn_pool = stack.enter_context(tc.tile_pool(name="xn", bufs=2))
-        work = stack.enter_context(tc.tile_pool(name="work", bufs=3))
-        plane_pool = stack.enter_context(tc.tile_pool(name="planes", bufs=2))
-        operand_pool = stack.enter_context(tc.tile_pool(name="operands", bufs=3))
+        work = stack.enter_context(tc.tile_pool(name="work", bufs=1))
+        operand_pool = stack.enter_context(tc.tile_pool(name="operands", bufs=4))
         result_pool = stack.enter_context(tc.tile_pool(name="results", bufs=4))
-        transposed_pool = stack.enter_context(tc.psum_pool(name="transposed", bufs=4))
+        transposed_pool = stack.enter_context(tc.psum_pool(name="transposed", bufs=SLOTS))
         acc_pool = stack.enter_context(tc.psum_pool(name="acc", bufs=ROW_TILES))
+        stack.enter_context(tc.manual_schedule())
 
-        def normalised_chunk(c):
-            x_rows = rows_pool.tile([P, ROW_TILES, FEATURES], BF16)
+        prep = {}
+
+        def load_rows(c):
+            prep["x"] = rows_pool.tile([P, ROW_TILES, FEATURES], BF16, name="x_rows")
             nc.sync.dma_start(
-                out=x_rows[:],
+                out=prep["x"][:],
                 in_=x[c * CHUNK : (c + 1) * CHUNK, :].rearrange("(t p) f -> p t f", p=P),
             )
+
+        def row_statistics():
             stats = small.tile([P, ROW_TILES, 6], F32)
-            mean_var = small.tile([P, ROW_TILES, 2], F32)
+            prep["mean_var"] = small.tile([P, ROW_TILES, 2], F32, name="mean_var")
             for t in range(ROW_TILES):
-                nc.vector.bn_stats(out=stats[:, t, :], in_=x_rows[:, t, :])
-                nc.vector.bn_aggr(out=mean_var[:, t, :], in_=stats[:, t, :])
-            var_eps = small.tile([P, ROW_TILES], F32)
-            nc.vector.tensor_scalar_add(out=var_eps[:], in0=mean_var[:, :, 1], scalar1=LN_EPS)
-            std = small.tile([P, ROW_TILES], F32)
-            nc.scalar.activation(out=std[:], in_=var_eps[:], func=FUNC.Sqrt)
+                nc.vector.bn_stats(out=stats[:, t, :], in_=prep["x"][:, t, :])
+                nc.vector.bn_aggr(out=prep["mean_var"][:, t, :], in_=stats[:, t, :])
+            prep["var_eps"] = small.tile([P, ROW_TILES], F32, name="var_eps")
+            nc.vector.tensor_scalar_add(
+                out=prep["var_eps"][:], in0=prep["mean_var"][:, :, 1], scalar1=LN_EPS
+            )
+
+        def row_std():
+            prep["std"] = small.tile([P, ROW_TILES], F32, name="std")
+            nc.scalar.activation(out=prep["std"][:], in_=prep["var_eps"][:], func=FUNC.Sqrt)
+
+        def row_rstd():
             rough = small.tile([P, ROW_TILES], F32)
-            nc.vector.reciprocal(out=rough[:], in_=std[:])
+            nc.vector.reciprocal(out=rough[:], in_=prep["std"][:])
             step = small.tile([P, ROW_TILES], F32)
             nc.vector.tensor_mul(out=step[:], in0=rough[:], in1=rough[:])
-            nc.vector.tensor_mul(out=step[:], in0=step[:], in1=var_eps[:])
+            nc.vector.tensor_mul(out=step[:], in0=step[:], in1=prep["var_eps"][:])
             nc.vector.tensor_scalar(
                 out=step[:], in0=step[:], scalar1=-0.5, scalar2=1.5, op0=ALU.mult, op1=ALU.add
             )
-            rstd = small.tile([P, ROW_TILES], F32)
-            nc.vector.tensor_mul(out=rstd[:], in0=rough[:], in1=step[:])
-            z = rows_pool.tile([P, ROW_TILES, SLOTS, P], F32)
-            for t in range(ROW_TILES):
-                nc.vector.tensor_scalar(
-                    out=z[:, t, :, :],
-                    in0=x_rows[:, t, :].rearrange("p (q s) -> p s q", s=SLOTS),
-                    scalar1=mean_var[:, t, 0:1],
-                    scalar2=rstd[:, t : t + 1],
-                    op0=ALU.subtract,
-                    op1=ALU.mult,
-                )
-            xn = xn_pool.tile([P, SLOTS, CHUNK], F32)
+            prep["rstd"] = small.tile([P, ROW_TILES], F32, name="rstd")
+            nc.vector.tensor_mul(out=prep["rstd"][:], in0=rough[:], in1=step[:])
+            prep["z"] = rows_pool.tile([P, ROW_TILES, SLOTS, P], F32, name="z", bufs=1)
+
+        def normalise(t):
+            nc.vector.tensor_scalar(
+                out=prep["z"][:, t, :, :],
+                in0=prep["x"][:, t, :].rearrange("p (q s) -> p s q", s=SLOTS),
+                scalar1=prep["mean_var"][:, t, 0:1],
+                scalar2=prep["rstd"][:, t : t + 1],
+                op0=ALU.subtract,
+                op1=ALU.mult,
+            )
+
+        def transpose_rows():
+            prep["z_t"] = []
             for s in range(SLOTS):
                 z_t = transposed_pool.tile([P, CHUNK], F32)
                 for t in range(ROW_TILES):
-                    nc.tensor.transpose(z_t[:, t * P : (t + 1) * P], z[:, t, s, :], identity[:])
+                    nc.tensor.transpose(
+                        z_t[:, t * P : (t + 1) * P], prep["z"][:, t, s, :], identity[:]
+                    )
+                prep["z_t"].append(z_t)
+
+        def scale_and_shift():
+            xn = xn_pool.tile([P, SLOTS, CHUNK], F32)
+            for s in range(SLOTS):
                 nc.scalar.activation(
                     out=xn[:, s, :],
-                    in_=z_t[:],
+                    in_=prep["z_t"][s][:],
                     func=FUNC.Identity,
                     scale=gamma[:, s : s + 1],
                     bias=beta[:, s : s + 1],
                 )
             return xn
 
-        def quantise_relu(planes):
+        def regroup_relu(planes, on_vector):
             grouped = operand_pool.tile([P, CHUNK, PACK], BF16, align_bytes=64)
-            nc.scalar.activation(
-                out=grouped[:], in_=planes.rearrange("p t r -> p r t"), func=FUNC.Relu
-            )
+            target = grouped[:].rearrange("p (b i) t -> p b t i", i=RUN)
+            source = planes.rearrange("p t (b i) -> p b t i", i=RUN)
+            if on_vector:
+                nc.vector.tensor_scalar_max(out=target, in0=source, scalar1=0.0)
+            else:
+                nc.scalar.activation(out=target, in_=source, func=FUNC.Relu)
+            return grouped
+
+        def quantise(grouped):
             codes = operand_pool.tile([P, CHUNK], U32, align_bytes=64)
             scales = operand_pool.tile([P, CHUNK], U8, align_bytes=64)
             nc.vector.quantize_mx(
@@ -129,7 +158,7 @@ def tile_kanlinear_pa_t_kernel(
             )
             return codes, scales
 
-        def multiply(acc, operand, weight_words, weight_scales, start, stop):
+        def multiply(acc, operand, weight_words, weight_scale_plane, start, stop):
             codes, scales = operand
             for t in range(ROW_TILES):
                 nc.tensor.matmul_mx(
@@ -137,24 +166,47 @@ def tile_kanlinear_pa_t_kernel(
                     lhsT=codes[:, t * P : (t + 1) * P].bitcast(FP8X4),
                     lhsT_scale=scales[:, t * P : (t + 1) * P],
                     rhs=weight_words.bitcast(FP8X4),
-                    rhs_scale=weight_scales,
+                    rhs_scale=weight_scale_plane,
                     start=start,
                     stop=stop,
                 )
 
-        identity = keep.tile([P, P], F32)
-        masks.make_identity(nc, identity[:])
+        def store_results(c, acc):
+            for t in range(ROW_TILES):
+                result = result_pool.tile([P, UNITS], F32)
+                nc.vector.tensor_add(out=result[:], in0=acc[t][:], in1=bias[:])
+                first_row = c * CHUNK + t * P
+                nc.sync.dma_start(out=out[first_row : first_row + P, :], in_=result[:])
+
+        load_rows(0)
         gamma_bf = keep.tile([P, SLOTS], BF16)
         beta_bf = keep.tile([P, SLOTS], BF16)
         knot_bf = keep.tile([P, SLOTS, KNOTS], BF16)
         nc.sync.dma_start(out=gamma_bf[:], in_=ln_gamma.rearrange("(p s) -> p s", s=SLOTS))
         nc.sync.dma_start(out=beta_bf[:], in_=ln_beta.rearrange("(p s) -> p s", s=SLOTS))
         nc.sync.dma_start(out=knot_bf[:], in_=grid.rearrange("o (p s) k -> (o p) s k", s=SLOTS))
+        identity = keep.tile([P, P], F32)
+        masks.make_identity(nc, identity[:])
+        one = keep.tile([P, 1], F32)
+        nc.vector.memset(one[:], 1.0)
+        nc.scalar.activation(out=one[:], in_=one[:], func=FUNC.Sqrt)
+        weight_scales = keep.tile([P, SHARES + 1, UNITS], U8, align_bytes=64)
+        nc.vector.memset(weight_scales[:].bitcast(I32), 0)
+        spline_words = keep.tile([P, WORDS, SHARES, UNITS], I32, align_bytes=64)
+        nc.vector.memset(spline_words[:], 0)
+
         gamma = keep.tile([P, SLOTS], F32)
         beta = keep.tile([P, SLOTS], F32)
         nc.vector.tensor_copy(out=gamma[:], in_=gamma_bf[:])
         nc.vector.tensor_copy(out=beta[:], in_=beta_bf[:])
-        xn_next = normalised_chunk(0)
+        row_statistics()
+        row_std()
+        row_rstd()
+        for t in range(ROW_TILES):
+            normalise(t)
+        transpose_rows()
+        xn = {0: scale_and_shift()}
+        load_rows(1)
 
         knot = keep.tile([P, SLOTS, KNOTS], F32)
         nc.vector.tensor_copy(out=knot[:], in_=knot_bf[:])
@@ -189,8 +241,6 @@ def tile_kanlinear_pa_t_kernel(
         bias = keep.tile([P, UNITS], F32)
         nc.vector.tensor_copy(out=bias[:], in_=bias_bf[:])
 
-        weight_scales = keep.tile([P, SHARES + 1, UNITS], U8, align_bytes=64)
-        nc.vector.memset(weight_scales[:].bitcast(I32), 0)
         spline_scale_rows = (
             spline_weight_scales.rearrange("g r n -> (g r) n")
             .bitcast(I32)
@@ -213,8 +263,6 @@ def tile_kanlinear_pa_t_kernel(
             out=base_words[:],
             in_=base_weight_words.rearrange("g p n t -> (g p) (n t)").bitcast(I32),
         )
-        spline_words = keep.tile([P, WORDS, SHARES, UNITS], I32, align_bytes=64)
-        nc.vector.memset(spline_words[:], 0)
         word_rows = (
             spline_weight_words.rearrange("g p n t -> (g p) (n t)")
             .bitcast(I32)
@@ -230,106 +278,120 @@ def tile_kanlinear_pa_t_kernel(
                         in_=word_rows[i][:, first:last, :],
                     )
 
-        for chunk in range(CHUNKS):
-            xn = xn_next
-            if chunk + 1 < CHUNKS:
-                xn_next = normalised_chunk(chunk + 1)
+        planes = keep.tile([P, SLOTS * BASES, CHUNK], BF16)
+        acc = {}
+        for r in range(ROUNDS + 2):
+            chunk, s = divmod(r, SLOTS)
+            computing = r < ROUNDS
+            preparing = computing and chunk + 1 < CHUNKS
 
-            acc = [
-                acc_pool.tile([P, UNITS], F32, name="acc%d" % t, tag="acc") for t in range(ROW_TILES)
-            ]
-            multiply(
-                acc,
-                quantise_relu(xn[:]),
-                base_words[:],
-                weight_scales[:, SHARES, :],
-                start=True,
-                stop=False,
-            )
-
-            planes = plane_pool.tile([P, SLOTS * BASES, CHUNK], BF16)
-            words_done = 0
-            for s in range(SLOTS):
-                v = xn[:, s, :]
-                cube = {}
-                fall_inner = {}
-                rise = {}
+            if computing:
+                v = xn[chunk][:, s, :]
+                square = work.tile([P, KNOTS, CHUNK], F32, bufs=2)
                 for i in range(KNOTS):
-                    square = work.tile([P, CHUNK], F32)
                     nc.scalar.activation(
-                        out=square[:],
+                        out=square[:, i, :],
                         in_=v,
                         func=FUNC.Square,
                         bias=neg_knot[:, s, i : i + 1],
                         scale=1.0,
                     )
-                    cube[i] = work.tile([P, CHUNK], F32, name="cube", tag="cube", bufs=4)
+                cube = work.tile([P, KNOTS, CHUNK], F32)
+                for i in range(KNOTS):
                     nc.vector.scalar_tensor_tensor(
-                        out=cube[i][:],
+                        out=cube[:, i, :],
                         in0=v,
                         scalar=knot[:, s, i : i + 1],
-                        in1=square[:],
+                        in1=square[:, i, :],
                         op0=ALU.subtract,
                         op1=ALU.mult,
                     )
-                    if 1 <= i <= BASES:
-                        j = i - 1
-                        rise_inner = work.tile([P, CHUNK], F32)
-                        nc.scalar.activation(
-                            out=rise_inner[:],
-                            in_=cube[i][:],
-                            func=FUNC.Relu,
-                            scale=c1[:, s, j : j + 1],
-                        )
-                        rise[j] = work.tile([P, CHUNK], BF16, name="rise", tag="rise", bufs=6)
-                        nc.vector.scalar_tensor_tensor(
-                            out=rise[j][:],
-                            in0=cube[j][:],
-                            scalar=c0[:, s, j : j + 1],
-                            in1=rise_inner[:],
-                            op0=ALU.mult,
-                            op1=ALU.subtract,
-                        )
-                    if 3 <= i < 3 + BASES:
-                        fall_inner[i] = work.tile(
-                            [P, CHUNK], F32, name="fall_inner", tag="fall_inner", bufs=4
-                        )
-                        nc.scalar.activation(
-                            out=fall_inner[i][:],
-                            in_=cube[i][:],
-                            func=FUNC.Relu,
-                            scale=neg_c3[:, s, i - 3 : i - 2],
-                        )
-                    if i >= 4:
-                        j = i - 4
-                        fall = work.tile([P, CHUNK], BF16)
-                        nc.vector.scalar_tensor_tensor(
-                            out=fall[:],
-                            in0=cube[i][:],
-                            scalar=neg_c4[:, s, j : j + 1],
-                            in1=fall_inner[i - 1][:],
-                            op0=ALU.mult,
-                            op1=ALU.subtract,
-                        )
-                        nc.vector.tensor_max(
-                            out=planes[:, BASES * s + j, :], in0=rise[j][:], in1=fall[:]
-                        )
-                words_ready = BASES * (s + 1) // PACK
-                for e in range(words_done, words_ready):
-                    operand = quantise_relu(planes[:, PACK * e : PACK * (e + 1), :])
-                    for c in range(SHARES):
-                        multiply(
-                            acc,
-                            operand,
-                            spline_words[:, e, c, :],
-                            weight_scales[:, c, :],
-                            start=False,
-                            stop=(e == WORDS - 1 and c == SHARES - 1),
-                        )
-                words_done = words_ready
 
-            for t in range(ROW_TILES):
-                result = result_pool.tile([P, UNITS], F32)
-                nc.vector.tensor_add(out=result[:], in0=acc[t][:], in1=bias[:])
-                first_row = chunk * CHUNK + t * P
-                nc.sync.dma_start(out=out[first_row : first_row + P, :], in_=result[:])
+            if preparing and s == 0:
+                row_statistics()
+            if preparing and s == 1:
+                row_rstd()
+                normalise(0)
+                normalise(1)
+            if preparing and s == 2:
+                normalise(2)
+                normalise(3)
+                transpose_rows()
+                if chunk + 2 < CHUNKS:
+                    load_rows(chunk + 2)
+            if s == 1 and chunk >= 1:
+                store_results(chunk - 1, acc[chunk - 1])
+
+            finished = []
+            if computing and s == 1:
+                finished.append((regroup_relu(xn[chunk][:], False), chunk, WORDS))
+            if 1 <= r <= ROUNDS:
+                last_chunk, last_s = divmod(r - 1, SLOTS)
+                for e in range(BASES * last_s // PACK, BASES * (last_s + 1) // PACK):
+                    word_planes = planes[:, PACK * e : PACK * (e + 1), :]
+                    finished.append((regroup_relu(word_planes, e == VECTOR_WORD), last_chunk, e))
+            if preparing and s == 3:
+                xn[chunk + 1] = scale_and_shift()
+            for grouped, c, e in finished:
+                operand = quantise(grouped)
+                if e == WORDS:
+                    acc[c] = [
+                        acc_pool.tile([P, UNITS], F32, name="acc%d" % t, tag="acc")
+                        for t in range(ROW_TILES)
+                    ]
+                    multiply(
+                        acc[c], operand, base_words[:], weight_scales[:, SHARES, :], True, False
+                    )
+                else:
+                    for share in range(SHARES):
+                        multiply(
+                            acc[c],
+                            operand,
+                            spline_words[:, e, share, :],
+                            weight_scales[:, share, :],
+                            False,
+                            e == WORDS - 1 and share == SHARES - 1,
+                        )
+
+            if computing:
+                rise_inner = work.tile([P, BASES, CHUNK], F32)
+                fall_inner = work.tile([P, BASES, CHUNK], F32)
+                for j in range(BASES):
+                    nc.scalar.activation(
+                        out=rise_inner[:, j, :],
+                        in_=cube[:, j + 1, :],
+                        func=FUNC.Relu,
+                        scale=c1[:, s, j : j + 1],
+                    )
+                for j in range(BASES):
+                    nc.scalar.activation(
+                        out=fall_inner[:, j, :],
+                        in_=cube[:, j + 3, :],
+                        func=FUNC.Relu,
+                        scale=neg_c3[:, s, j : j + 1],
+                    )
+                rise = work.tile([P, BASES, CHUNK], BF16)
+                fall = work.tile([P, BASES, CHUNK], BF16)
+                for j in range(BASES):
+                    nc.vector.scalar_tensor_tensor(
+                        out=rise[:, j, :],
+                        in0=cube[:, j, :],
+                        scalar=c0[:, s, j : j + 1],
+                        in1=rise_inner[:, j, :],
+                        op0=ALU.mult,
+                        op1=ALU.subtract,
+                    )
+                for j in range(BASES):
+                    nc.vector.scalar_tensor_tensor(
+                        out=fall[:, j, :],
+                        in0=cube[:, j + 4, :],
+                        scalar=neg_c4[:, s, j : j + 1],
+                        in1=fall_inner[:, j, :],
+                        op0=ALU.mult,
+                        op1=ALU.subtract,
+                    )
+                nc.vector.tensor_max(
+                    out=planes[:, BASES * s : BASES * (s + 1), :], in0=rise[:], in1=fall[:]
+                )
+            if preparing and s == 0:
+                row_std()

@@ -104,16 +104,24 @@ def tile_kanlinear_pa_t_kernel(
             )
             prep["rstd"] = small.tile([P, ROW_TILES], F32, name="rstd")
             nc.vector.tensor_mul(out=prep["rstd"][:], in0=rough[:], in1=step[:])
+            prep["shift"] = small.tile([P, ROW_TILES], F32, name="shift")
+            nc.vector.scalar_tensor_tensor(
+                out=prep["shift"][:],
+                in0=prep["mean_var"][:, :, 0],
+                scalar=-1.0,
+                in1=prep["rstd"][:],
+                op0=ALU.mult,
+                op1=ALU.mult,
+            )
             prep["z"] = rows_pool.tile([P, ROW_TILES, SLOTS, P], F32, name="z", bufs=1)
 
         def normalise(t):
-            nc.vector.tensor_scalar(
+            nc.scalar.activation(
                 out=prep["z"][:, t, :, :],
-                in0=prep["x"][:, t, :].rearrange("p (q s) -> p s q", s=SLOTS),
-                scalar1=prep["mean_var"][:, t, 0:1],
-                scalar2=prep["rstd"][:, t : t + 1],
-                op0=ALU.subtract,
-                op1=ALU.mult,
+                in_=prep["x"][:, t, :].rearrange("p (q s) -> p s q", s=SLOTS),
+                func=FUNC.Identity,
+                scale=prep["rstd"][:, t : t + 1],
+                bias=prep["shift"][:, t : t + 1],
             )
 
         def transpose_rows():
@@ -158,18 +166,19 @@ def tile_kanlinear_pa_t_kernel(
             )
             return codes, scales
 
-        def multiply(acc, operand, weight_words, weight_scale_plane, start, stop):
+        def multiply(acc, operand, weights, start, stop):
             codes, scales = operand
             for t in range(ROW_TILES):
-                nc.tensor.matmul_mx(
-                    out=acc[t][:],
-                    lhsT=codes[:, t * P : (t + 1) * P].bitcast(FP8X4),
-                    lhsT_scale=scales[:, t * P : (t + 1) * P],
-                    rhs=weight_words.bitcast(FP8X4),
-                    rhs_scale=weight_scale_plane,
-                    start=start,
-                    stop=stop,
-                )
+                for n, (words, scale_plane) in enumerate(weights):
+                    nc.tensor.matmul_mx(
+                        out=acc[t][:],
+                        lhsT=codes[:, t * P : (t + 1) * P].bitcast(FP8X4),
+                        lhsT_scale=scales[:, t * P : (t + 1) * P],
+                        rhs=words.bitcast(FP8X4),
+                        rhs_scale=scale_plane,
+                        start=start and n == 0,
+                        stop=stop and n == len(weights) - 1,
+                    )
 
         def store_results(c, acc):
             for t in range(ROW_TILES):
@@ -311,14 +320,6 @@ def tile_kanlinear_pa_t_kernel(
                 row_statistics()
             if preparing and s == 1:
                 row_rstd()
-                normalise(0)
-                normalise(1)
-            if preparing and s == 2:
-                normalise(2)
-                normalise(3)
-                transpose_rows()
-                if chunk + 2 < CHUNKS:
-                    load_rows(chunk + 2)
             if s == 1 and chunk >= 1:
                 store_results(chunk - 1, acc[chunk - 1])
 
@@ -329,7 +330,11 @@ def tile_kanlinear_pa_t_kernel(
                 last_chunk, last_s = divmod(r - 1, SLOTS)
                 for e in range(BASES * last_s // PACK, BASES * (last_s + 1) // PACK):
                     word_planes = planes[:, PACK * e : PACK * (e + 1), :]
-                    finished.append((regroup_relu(word_planes, e == VECTOR_WORD), last_chunk, e))
+                    on_vector = e == VECTOR_WORD or (e == WORDS - 1 and not computing)
+                    finished.append((regroup_relu(word_planes, on_vector), last_chunk, e))
+            if preparing and s == 2:
+                for t in range(ROW_TILES):
+                    normalise(t)
             if preparing and s == 3:
                 xn[chunk + 1] = scale_and_shift()
             for grouped, c, e in finished:
@@ -340,18 +345,18 @@ def tile_kanlinear_pa_t_kernel(
                         for t in range(ROW_TILES)
                     ]
                     multiply(
-                        acc[c], operand, base_words[:], weight_scales[:, SHARES, :], True, False
+                        acc[c], operand, [(base_words[:], weight_scales[:, SHARES, :])], True, False
                     )
                 else:
-                    for share in range(SHARES):
-                        multiply(
-                            acc[c],
-                            operand,
-                            spline_words[:, e, share, :],
-                            weight_scales[:, share, :],
-                            False,
-                            e == WORDS - 1 and share == SHARES - 1,
-                        )
+                    shares = [
+                        (spline_words[:, e, share, :], weight_scales[:, share, :])
+                        for share in range(SHARES)
+                    ]
+                    multiply(acc[c], operand, shares, False, e == WORDS - 1)
+            if preparing and s == 2:
+                transpose_rows()
+                if chunk + 2 < CHUNKS:
+                    load_rows(chunk + 2)
 
             if computing:
                 rise_inner = work.tile([P, BASES, CHUNK], F32)

@@ -67,7 +67,6 @@ def tile_kanlinear_pa_t_kernel(
         result_pool = stack.enter_context(tc.tile_pool(name="results", bufs=4))
         transposed_pool = stack.enter_context(tc.psum_pool(name="transposed", bufs=SLOTS))
         acc_pool = stack.enter_context(tc.psum_pool(name="acc", bufs=ROW_TILES))
-        stack.enter_context(tc.manual_schedule())
 
         prep = {}
 
@@ -104,24 +103,16 @@ def tile_kanlinear_pa_t_kernel(
             )
             prep["rstd"] = small.tile([P, ROW_TILES], F32, name="rstd")
             nc.vector.tensor_mul(out=prep["rstd"][:], in0=rough[:], in1=step[:])
-            prep["shift"] = small.tile([P, ROW_TILES], F32, name="shift")
-            nc.vector.scalar_tensor_tensor(
-                out=prep["shift"][:],
-                in0=prep["mean_var"][:, :, 0],
-                scalar=-1.0,
-                in1=prep["rstd"][:],
-                op0=ALU.mult,
-                op1=ALU.mult,
-            )
             prep["z"] = rows_pool.tile([P, ROW_TILES, SLOTS, P], F32, name="z", bufs=1)
 
         def normalise(t):
-            nc.scalar.activation(
+            nc.vector.tensor_scalar(
                 out=prep["z"][:, t, :, :],
-                in_=prep["x"][:, t, :].rearrange("p (q s) -> p s q", s=SLOTS),
-                func=FUNC.Identity,
-                scale=prep["rstd"][:, t : t + 1],
-                bias=prep["shift"][:, t : t + 1],
+                in0=prep["x"][:, t, :].rearrange("p (q s) -> p s q", s=SLOTS),
+                scalar1=prep["mean_var"][:, t, 0:1],
+                scalar2=prep["rstd"][:, t : t + 1],
+                op0=ALU.subtract,
+                op1=ALU.mult,
             )
 
         def transpose_rows():
@@ -166,19 +157,18 @@ def tile_kanlinear_pa_t_kernel(
             )
             return codes, scales
 
-        def multiply(acc, operand, weights, start, stop):
+        def multiply(acc, operand, weight_words, weight_scale_plane, start, stop):
             codes, scales = operand
             for t in range(ROW_TILES):
-                for n, (words, scale_plane) in enumerate(weights):
-                    nc.tensor.matmul_mx(
-                        out=acc[t][:],
-                        lhsT=codes[:, t * P : (t + 1) * P].bitcast(FP8X4),
-                        lhsT_scale=scales[:, t * P : (t + 1) * P],
-                        rhs=words.bitcast(FP8X4),
-                        rhs_scale=scale_plane,
-                        start=start and n == 0,
-                        stop=stop and n == len(weights) - 1,
-                    )
+                nc.tensor.matmul_mx(
+                    out=acc[t][:],
+                    lhsT=codes[:, t * P : (t + 1) * P].bitcast(FP8X4),
+                    lhsT_scale=scales[:, t * P : (t + 1) * P],
+                    rhs=weight_words.bitcast(FP8X4),
+                    rhs_scale=weight_scale_plane,
+                    start=start,
+                    stop=stop,
+                )
 
         def store_results(c, acc):
             for t in range(ROW_TILES):
@@ -320,6 +310,14 @@ def tile_kanlinear_pa_t_kernel(
                 row_statistics()
             if preparing and s == 1:
                 row_rstd()
+                normalise(0)
+                normalise(1)
+            if preparing and s == 2:
+                normalise(2)
+                normalise(3)
+                transpose_rows()
+                if chunk + 2 < CHUNKS:
+                    load_rows(chunk + 2)
             if s == 1 and chunk >= 1:
                 store_results(chunk - 1, acc[chunk - 1])
 
@@ -330,11 +328,7 @@ def tile_kanlinear_pa_t_kernel(
                 last_chunk, last_s = divmod(r - 1, SLOTS)
                 for e in range(BASES * last_s // PACK, BASES * (last_s + 1) // PACK):
                     word_planes = planes[:, PACK * e : PACK * (e + 1), :]
-                    on_vector = e == VECTOR_WORD or (e == WORDS - 1 and not computing)
-                    finished.append((regroup_relu(word_planes, on_vector), last_chunk, e))
-            if preparing and s == 2:
-                for t in range(ROW_TILES):
-                    normalise(t)
+                    finished.append((regroup_relu(word_planes, e == VECTOR_WORD), last_chunk, e))
             if preparing and s == 3:
                 xn[chunk + 1] = scale_and_shift()
             for grouped, c, e in finished:
@@ -345,18 +339,18 @@ def tile_kanlinear_pa_t_kernel(
                         for t in range(ROW_TILES)
                     ]
                     multiply(
-                        acc[c], operand, [(base_words[:], weight_scales[:, SHARES, :])], True, False
+                        acc[c], operand, base_words[:], weight_scales[:, SHARES, :], True, False
                     )
                 else:
-                    shares = [
-                        (spline_words[:, e, share, :], weight_scales[:, share, :])
-                        for share in range(SHARES)
-                    ]
-                    multiply(acc[c], operand, shares, False, e == WORDS - 1)
-            if preparing and s == 2:
-                transpose_rows()
-                if chunk + 2 < CHUNKS:
-                    load_rows(chunk + 2)
+                    for share in range(SHARES):
+                        multiply(
+                            acc[c],
+                            operand,
+                            spline_words[:, e, share, :],
+                            weight_scales[:, share, :],
+                            False,
+                            e == WORDS - 1 and share == SHARES - 1,
+                        )
 
             if computing:
                 rise_inner = work.tile([P, BASES, CHUNK], F32)

@@ -157,18 +157,19 @@ def tile_kanlinear_pa_t_kernel(
             )
             return codes, scales
 
-        def multiply(acc, operand, weight_words, weight_scale_plane, start, stop):
+        def multiply(acc, operand, weights, start, stop):
             codes, scales = operand
             for t in range(ROW_TILES):
-                nc.tensor.matmul_mx(
-                    out=acc[t][:],
-                    lhsT=codes[:, t * P : (t + 1) * P].bitcast(FP8X4),
-                    lhsT_scale=scales[:, t * P : (t + 1) * P],
-                    rhs=weight_words.bitcast(FP8X4),
-                    rhs_scale=weight_scale_plane,
-                    start=start,
-                    stop=stop,
-                )
+                for n, (words, scale_plane) in enumerate(weights):
+                    nc.tensor.matmul_mx(
+                        out=acc[t][:],
+                        lhsT=codes[:, t * P : (t + 1) * P].bitcast(FP8X4),
+                        lhsT_scale=scales[:, t * P : (t + 1) * P],
+                        rhs=words.bitcast(FP8X4),
+                        rhs_scale=scale_plane,
+                        start=start and n == 0,
+                        stop=stop and n == len(weights) - 1,
+                    )
 
         def store_results(c, acc):
             for t in range(ROW_TILES):
@@ -192,7 +193,8 @@ def tile_kanlinear_pa_t_kernel(
         weight_scales = keep.tile([P, SHARES + 1, UNITS], U8, align_bytes=64)
         nc.vector.memset(weight_scales[:].bitcast(I32), 0)
         spline_words = keep.tile([P, WORDS, SHARES, UNITS], I32, align_bytes=64)
-        nc.vector.memset(spline_words[:], 0)
+        for e in range(WORDS):
+            nc.gpsimd.memset(spline_words[:, e, :, :].bitcast(F32), 0.0)
 
         gamma = keep.tile([P, SLOTS], F32)
         beta = keep.tile([P, SLOTS], F32)
@@ -328,7 +330,8 @@ def tile_kanlinear_pa_t_kernel(
                 last_chunk, last_s = divmod(r - 1, SLOTS)
                 for e in range(BASES * last_s // PACK, BASES * (last_s + 1) // PACK):
                     word_planes = planes[:, PACK * e : PACK * (e + 1), :]
-                    finished.append((regroup_relu(word_planes, e == VECTOR_WORD), last_chunk, e))
+                    on_vector = e == VECTOR_WORD or (e == WORDS - 1 and not computing)
+                    finished.append((regroup_relu(word_planes, on_vector), last_chunk, e))
             if preparing and s == 3:
                 xn[chunk + 1] = scale_and_shift()
             for grouped, c, e in finished:
@@ -339,18 +342,14 @@ def tile_kanlinear_pa_t_kernel(
                         for t in range(ROW_TILES)
                     ]
                     multiply(
-                        acc[c], operand, base_words[:], weight_scales[:, SHARES, :], True, False
+                        acc[c], operand, [(base_words[:], weight_scales[:, SHARES, :])], True, False
                     )
                 else:
-                    for share in range(SHARES):
-                        multiply(
-                            acc[c],
-                            operand,
-                            spline_words[:, e, share, :],
-                            weight_scales[:, share, :],
-                            False,
-                            e == WORDS - 1 and share == SHARES - 1,
-                        )
+                    shares = [
+                        (spline_words[:, e, share, :], weight_scales[:, share, :])
+                        for share in range(SHARES)
+                    ]
+                    multiply(acc[c], operand, shares, False, e == WORDS - 1)
 
             if computing:
                 rise_inner = work.tile([P, BASES, CHUNK], F32)

@@ -30,7 +30,8 @@ ROW_TILES = CHUNK // P
 CHUNKS = ROWS // CHUNK
 ROUNDS = CHUNKS * SLOTS
 RUN = 4
-VECTOR_WORD = 3
+MATCHED_RISE = (0, 2, 4)
+MATCHED_FALL = (3, 5)
 
 FLOPS = 2 * ROWS * (FEATURES + FEATURES * BASES) * UNITS
 
@@ -103,16 +104,24 @@ def tile_kanlinear_pa_t_kernel(
             )
             prep["rstd"] = small.tile([P, ROW_TILES], F32, name="rstd")
             nc.vector.tensor_mul(out=prep["rstd"][:], in0=rough[:], in1=step[:])
+            prep["shift"] = small.tile([P, ROW_TILES], F32, name="shift")
+            nc.vector.scalar_tensor_tensor(
+                out=prep["shift"][:],
+                in0=prep["mean_var"][:, :, 0],
+                scalar=-1.0,
+                in1=prep["rstd"][:],
+                op0=ALU.mult,
+                op1=ALU.mult,
+            )
             prep["z"] = rows_pool.tile([P, ROW_TILES, SLOTS, P], F32, name="z", bufs=1)
 
         def normalise(t):
-            nc.vector.tensor_scalar(
+            nc.scalar.activation(
                 out=prep["z"][:, t, :, :],
-                in0=prep["x"][:, t, :].rearrange("p (q s) -> p s q", s=SLOTS),
-                scalar1=prep["mean_var"][:, t, 0:1],
-                scalar2=prep["rstd"][:, t : t + 1],
-                op0=ALU.subtract,
-                op1=ALU.mult,
+                in_=prep["x"][:, t, :].rearrange("p (q s) -> p s q", s=SLOTS),
+                func=FUNC.Identity,
+                scale=prep["rstd"][:, t : t + 1],
+                bias=prep["shift"][:, t : t + 1],
             )
 
         def transpose_rows():
@@ -237,6 +246,28 @@ def tile_kanlinear_pa_t_kernel(
             out=neg_c3[:], in0=neg_c3[:], scalar=-1.0, in1=spans(4, 0), op0=ALU.mult, op1=ALU.mult
         )
 
+        scale = keep.tile([P, SLOTS, KNOTS], F32)
+        nc.vector.tensor_copy(out=scale[:, :, 0:6:2], in_=c0[:, :, 0:6:2])
+        nc.vector.tensor_copy(out=scale[:, :, 1:6:2], in_=c1[:, :, 0:6:2])
+        nc.vector.tensor_scalar_mul(out=scale[:, :, 6:10:2], in0=neg_c3[:, :, 3:6:2], scalar1=-1.0)
+        nc.vector.tensor_scalar_mul(out=scale[:, :, 7:10:2], in0=neg_c4[:, :, 3:6:2], scalar1=-1.0)
+        rough_root = keep.tile([P, SLOTS, KNOTS], F32)
+        nc.scalar.activation(out=rough_root[:], in_=scale[:], func=FUNC.Sqrt)
+        root = keep.tile([P, SLOTS, KNOTS], F32)
+        nc.vector.reciprocal(out=root[:], in_=rough_root[:])
+        nc.vector.tensor_mul(out=root[:], in0=root[:], in1=scale[:])
+        nc.vector.tensor_add(out=root[:], in0=root[:], in1=rough_root[:])
+        nc.vector.tensor_scalar_mul(out=root[:], in0=root[:], scalar1=0.5)
+        neg_root_knot = keep.tile([P, SLOTS, KNOTS], F32)
+        nc.vector.tensor_mul(out=neg_root_knot[:], in0=root[:], in1=neg_knot[:])
+        unscale = keep.tile([P, SLOTS, KNOTS], F32)
+        nc.vector.tensor_mul(out=unscale[:], in0=root[:], in1=root[:])
+        nc.vector.reciprocal(out=unscale[:], in_=unscale[:])
+        nc.vector.tensor_mul(out=c0[:], in0=c0[:], in1=unscale[:, :, 0:6])
+        nc.vector.tensor_mul(out=c1[:], in0=c1[:], in1=unscale[:, :, 1:7])
+        nc.vector.tensor_mul(out=neg_c3[:], in0=neg_c3[:], in1=unscale[:, :, 3:9])
+        nc.vector.tensor_mul(out=neg_c4[:], in0=neg_c4[:], in1=unscale[:, :, 4:10])
+
         bias_bf = keep.tile([P, UNITS], BF16)
         nc.sync.dma_start(out=bias_bf[:], in_=base_bias.partition_broadcast(P))
         bias = keep.tile([P, UNITS], F32)
@@ -294,8 +325,8 @@ def tile_kanlinear_pa_t_kernel(
                         out=square[:, i, :],
                         in_=v,
                         func=FUNC.Square,
-                        bias=neg_knot[:, s, i : i + 1],
-                        scale=1.0,
+                        bias=neg_root_knot[:, s, i : i + 1],
+                        scale=root[:, s, i : i + 1],
                     )
                 cube = work.tile([P, KNOTS, CHUNK], F32)
                 for i in range(KNOTS):
@@ -330,7 +361,7 @@ def tile_kanlinear_pa_t_kernel(
                 last_chunk, last_s = divmod(r - 1, SLOTS)
                 for e in range(BASES * last_s // PACK, BASES * (last_s + 1) // PACK):
                     word_planes = planes[:, PACK * e : PACK * (e + 1), :]
-                    on_vector = e == VECTOR_WORD or (e == WORDS - 1 and not computing)
+                    on_vector = e == WORDS - 1 and not computing
                     finished.append((regroup_relu(word_planes, on_vector), last_chunk, e))
             if preparing and s == 3:
                 xn[chunk + 1] = scale_and_shift()
@@ -355,6 +386,8 @@ def tile_kanlinear_pa_t_kernel(
                 rise_inner = work.tile([P, BASES, CHUNK], F32)
                 fall_inner = work.tile([P, BASES, CHUNK], F32)
                 for j in range(BASES):
+                    if j in MATCHED_RISE:
+                        continue
                     nc.scalar.activation(
                         out=rise_inner[:, j, :],
                         in_=cube[:, j + 1, :],
@@ -362,6 +395,8 @@ def tile_kanlinear_pa_t_kernel(
                         scale=c1[:, s, j : j + 1],
                     )
                 for j in range(BASES):
+                    if j in MATCHED_FALL:
+                        continue
                     nc.scalar.activation(
                         out=fall_inner[:, j, :],
                         in_=cube[:, j + 3, :],
@@ -371,6 +406,17 @@ def tile_kanlinear_pa_t_kernel(
                 rise = work.tile([P, BASES, CHUNK], BF16)
                 fall = work.tile([P, BASES, CHUNK], BF16)
                 for j in range(BASES):
+                    if j in MATCHED_RISE:
+                        nc.vector.scalar_tensor_tensor(
+                            out=rise[:, j, :],
+                            in0=cube[:, j + 1, :],
+                            scalar=0.0,
+                            in1=cube[:, j, :],
+                            op0=ALU.max,
+                            op1=ALU.subtract,
+                            reverse1=True,
+                        )
+                        continue
                     nc.vector.scalar_tensor_tensor(
                         out=rise[:, j, :],
                         in0=cube[:, j, :],
@@ -380,6 +426,16 @@ def tile_kanlinear_pa_t_kernel(
                         op1=ALU.subtract,
                     )
                 for j in range(BASES):
+                    if j in MATCHED_FALL:
+                        nc.vector.scalar_tensor_tensor(
+                            out=fall[:, j, :],
+                            in0=cube[:, j + 3, :],
+                            scalar=0.0,
+                            in1=cube[:, j + 4, :],
+                            op0=ALU.min,
+                            op1=ALU.subtract,
+                        )
+                        continue
                     nc.vector.scalar_tensor_tensor(
                         out=fall[:, j, :],
                         in0=cube[:, j + 4, :],

@@ -30,8 +30,10 @@ ROW_TILES = CHUNK // P
 CHUNKS = ROWS // CHUNK
 ROUNDS = CHUNKS * SLOTS
 RUN = 4
-MATCHED_RISE = (0, 2, 4)
-MATCHED_FALL = (3, 5)
+GPSIMD_KNOTS = (0, 9)
+VECTOR_KNOTS = (2, 3, 4, 5, 6, 7, 1, 8)
+SINGLE_RISE = (1, 3, 5)
+SINGLE_FALL = (0, 1, 2, 4)
 
 FLOPS = 2 * ROWS * (FEATURES + FEATURES * BASES) * UNITS
 
@@ -66,7 +68,8 @@ def tile_kanlinear_pa_t_kernel(
         work = stack.enter_context(tc.tile_pool(name="work", bufs=1))
         operand_pool = stack.enter_context(tc.tile_pool(name="operands", bufs=4))
         result_pool = stack.enter_context(tc.tile_pool(name="results", bufs=4))
-        transposed_pool = stack.enter_context(tc.psum_pool(name="transposed", bufs=SLOTS))
+        transposed_pool = stack.enter_context(tc.psum_pool(name="transposed", bufs=2))
+        v_pool = stack.enter_context(tc.psum_pool(name="v", bufs=2))
         acc_pool = stack.enter_context(tc.psum_pool(name="acc", bufs=ROW_TILES))
 
         prep = {}
@@ -124,27 +127,22 @@ def tile_kanlinear_pa_t_kernel(
                 bias=prep["shift"][:, t : t + 1],
             )
 
-        def transpose_rows():
-            prep["z_t"] = []
-            for s in range(SLOTS):
-                z_t = transposed_pool.tile([P, CHUNK], F32)
-                for t in range(ROW_TILES):
-                    nc.tensor.transpose(
-                        z_t[:, t * P : (t + 1) * P], prep["z"][:, t, s, :], identity[:]
-                    )
-                prep["z_t"].append(z_t)
+        def bring_xn(xn, s):
+            z_t = transposed_pool.tile([P, CHUNK], F32)
+            for t in range(ROW_TILES):
+                nc.tensor.transpose(z_t[:, t * P : (t + 1) * P], prep["z"][:, t, s, :], identity[:])
+            nc.scalar.activation(
+                out=xn[:, s, :],
+                in_=z_t[:],
+                func=FUNC.Identity,
+                scale=gamma[:, s : s + 1],
+                bias=beta[:, s : s + 1],
+            )
 
-        def scale_and_shift():
-            xn = xn_pool.tile([P, SLOTS, CHUNK], F32)
-            for s in range(SLOTS):
-                nc.scalar.activation(
-                    out=xn[:, s, :],
-                    in_=prep["z_t"][s][:],
-                    func=FUNC.Identity,
-                    scale=gamma[:, s : s + 1],
-                    bias=beta[:, s : s + 1],
-                )
-            return xn
+        def copy_to_psum(v):
+            v_psum = v_pool.tile([P, CHUNK], F32)
+            nc.tensor.matmul(v_psum[:], lhsT=identity[:], rhs=v, start=True, stop=True)
+            return v_psum
 
         def regroup_relu(planes, on_vector):
             grouped = operand_pool.tile([P, CHUNK, PACK], BF16, align_bytes=64)
@@ -214,8 +212,9 @@ def tile_kanlinear_pa_t_kernel(
         row_rstd()
         for t in range(ROW_TILES):
             normalise(t)
-        transpose_rows()
-        xn = {0: scale_and_shift()}
+        xn = {0: xn_pool.tile([P, SLOTS, CHUNK], F32, name="xn_tile")}
+        for s in range(SLOTS):
+            bring_xn(xn[0], s)
         load_rows(1)
 
         knot = keep.tile([P, SLOTS, KNOTS], F32)
@@ -312,6 +311,7 @@ def tile_kanlinear_pa_t_kernel(
 
         planes = keep.tile([P, SLOTS * BASES, CHUNK], BF16)
         acc = {}
+        v_next = copy_to_psum(xn[0][:, 0, :])
         for r in range(ROUNDS + 2):
             chunk, s = divmod(r, SLOTS)
             computing = r < ROUNDS
@@ -319,8 +319,9 @@ def tile_kanlinear_pa_t_kernel(
 
             if computing:
                 v = xn[chunk][:, s, :]
+                v_psum = v_next
                 square = work.tile([P, KNOTS, CHUNK], F32, bufs=2)
-                for i in range(KNOTS):
+                for i in GPSIMD_KNOTS + VECTOR_KNOTS:
                     nc.scalar.activation(
                         out=square[:, i, :],
                         in_=v,
@@ -329,10 +330,20 @@ def tile_kanlinear_pa_t_kernel(
                         scale=root[:, s, i : i + 1],
                     )
                 cube = work.tile([P, KNOTS, CHUNK], F32)
-                for i in range(KNOTS):
-                    nc.vector.scalar_tensor_tensor(
+                for i in GPSIMD_KNOTS:
+                    nc.gpsimd.tensor_scalar(
                         out=cube[:, i, :],
                         in0=v,
+                        scalar1=1.0,
+                        scalar2=neg_knot[:, s, i : i + 1],
+                        op0=ALU.mult,
+                        op1=ALU.add,
+                    )
+                    nc.gpsimd.tensor_mul(out=cube[:, i, :], in0=cube[:, i, :], in1=square[:, i, :])
+                for i in VECTOR_KNOTS:
+                    nc.vector.scalar_tensor_tensor(
+                        out=cube[:, i, :],
+                        in0=v_psum[:],
                         scalar=knot[:, s, i : i + 1],
                         in1=square[:, i, :],
                         op0=ALU.subtract,
@@ -348,7 +359,9 @@ def tile_kanlinear_pa_t_kernel(
             if preparing and s == 2:
                 normalise(2)
                 normalise(3)
-                transpose_rows()
+                xn[chunk + 1] = xn_pool.tile([P, SLOTS, CHUNK], F32, name="xn_tile")
+                bring_xn(xn[chunk + 1], 0)
+                bring_xn(xn[chunk + 1], 1)
                 if chunk + 2 < CHUNKS:
                     load_rows(chunk + 2)
             if s == 1 and chunk >= 1:
@@ -364,7 +377,11 @@ def tile_kanlinear_pa_t_kernel(
                     on_vector = e == WORDS - 1 and not computing
                     finished.append((regroup_relu(word_planes, on_vector), last_chunk, e))
             if preparing and s == 3:
-                xn[chunk + 1] = scale_and_shift()
+                bring_xn(xn[chunk + 1], 2)
+                bring_xn(xn[chunk + 1], 3)
+            if r + 1 < ROUNDS:
+                next_chunk, next_s = divmod(r + 1, SLOTS)
+                v_next = copy_to_psum(xn[next_chunk][:, next_s, :])
             for grouped, c, e in finished:
                 operand = quantise(grouped)
                 if e == WORDS:
@@ -385,38 +402,24 @@ def tile_kanlinear_pa_t_kernel(
             if computing:
                 rise_inner = work.tile([P, BASES, CHUNK], F32)
                 fall_inner = work.tile([P, BASES, CHUNK], F32)
-                for j in range(BASES):
-                    if j in MATCHED_RISE:
-                        continue
-                    nc.scalar.activation(
-                        out=rise_inner[:, j, :],
-                        in_=cube[:, j + 1, :],
-                        func=FUNC.Relu,
-                        scale=c1[:, s, j : j + 1],
-                    )
-                for j in range(BASES):
-                    if j in MATCHED_FALL:
-                        continue
-                    nc.scalar.activation(
-                        out=fall_inner[:, j, :],
-                        in_=cube[:, j + 3, :],
-                        func=FUNC.Relu,
-                        scale=neg_c3[:, s, j : j + 1],
-                    )
+                for i in VECTOR_KNOTS:
+                    if i - 1 in SINGLE_RISE:
+                        nc.scalar.activation(
+                            out=rise_inner[:, i - 1, :],
+                            in_=cube[:, i, :],
+                            func=FUNC.Relu,
+                            scale=c1[:, s, i - 1 : i],
+                        )
+                    if i - 3 in SINGLE_FALL:
+                        nc.scalar.activation(
+                            out=fall_inner[:, i - 3, :],
+                            in_=cube[:, i, :],
+                            func=FUNC.Relu,
+                            scale=neg_c3[:, s, i - 3 : i - 2],
+                        )
                 rise = work.tile([P, BASES, CHUNK], BF16)
                 fall = work.tile([P, BASES, CHUNK], BF16)
-                for j in range(BASES):
-                    if j in MATCHED_RISE:
-                        nc.vector.scalar_tensor_tensor(
-                            out=rise[:, j, :],
-                            in0=cube[:, j + 1, :],
-                            scalar=0.0,
-                            in1=cube[:, j, :],
-                            op0=ALU.max,
-                            op1=ALU.subtract,
-                            reverse1=True,
-                        )
-                        continue
+                for j in SINGLE_RISE:
                     nc.vector.scalar_tensor_tensor(
                         out=rise[:, j, :],
                         in0=cube[:, j, :],
@@ -425,17 +428,7 @@ def tile_kanlinear_pa_t_kernel(
                         op0=ALU.mult,
                         op1=ALU.subtract,
                     )
-                for j in range(BASES):
-                    if j in MATCHED_FALL:
-                        nc.vector.scalar_tensor_tensor(
-                            out=fall[:, j, :],
-                            in0=cube[:, j + 3, :],
-                            scalar=0.0,
-                            in1=cube[:, j + 4, :],
-                            op0=ALU.min,
-                            op1=ALU.subtract,
-                        )
-                        continue
+                for j in SINGLE_FALL:
                     nc.vector.scalar_tensor_tensor(
                         out=fall[:, j, :],
                         in0=cube[:, j + 4, :],
@@ -444,6 +437,23 @@ def tile_kanlinear_pa_t_kernel(
                         op0=ALU.mult,
                         op1=ALU.subtract,
                     )
+                nc.vector.scalar_tensor_tensor(
+                    out=rise[:, 0:6:2, :],
+                    in0=cube[:, 1:6:2, :],
+                    scalar=0.0,
+                    in1=cube[:, 0:6:2, :],
+                    op0=ALU.max,
+                    op1=ALU.subtract,
+                    reverse1=True,
+                )
+                nc.vector.scalar_tensor_tensor(
+                    out=fall[:, 3:6:2, :],
+                    in0=cube[:, 6:10:2, :],
+                    scalar=0.0,
+                    in1=cube[:, 7:10:2, :],
+                    op0=ALU.min,
+                    op1=ALU.subtract,
+                )
                 nc.vector.tensor_max(
                     out=planes[:, BASES * s : BASES * (s + 1), :], in0=rise[:], in1=fall[:]
                 )

@@ -32,18 +32,17 @@ ROUNDS = CHUNKS * SLOTS
 RUN = 4
 GPSIMD_KNOTS = (0, 9)
 VECTOR_KNOTS = (2, 3, 4, 5, 6, 7, 1, 8)
+SQUARE_ORDER = (2, 3, 0, 4, 9, 5, 6, 7, 1, 8)
 SINGLE_RISE = (1, 3, 5)
 SINGLE_FALL = (0, 1, 2, 4)
 
 FLOPS = 2 * ROWS * (FEATURES + FEATURES * BASES) * UNITS
 
 
-def product(nc, pool, name, factors):
-    result = pool.tile([P, SLOTS, BASES], F32, name=name)
-    nc.vector.tensor_mul(out=result[:], in0=factors[0], in1=factors[1])
+def product(nc, result, factors):
+    nc.vector.tensor_mul(out=result, in0=factors[0], in1=factors[1])
     for factor in factors[2:]:
-        nc.vector.tensor_mul(out=result[:], in0=result[:], in1=factor)
-    return result
+        nc.vector.tensor_mul(out=result, in0=result, in1=factor)
 
 
 def tile_kanlinear_pa_t_kernel(
@@ -76,10 +75,9 @@ def tile_kanlinear_pa_t_kernel(
 
         def load_rows(c):
             prep["x"] = rows_pool.tile([P, ROW_TILES, FEATURES], BF16, name="x_rows")
-            nc.sync.dma_start(
-                out=prep["x"][:],
-                in_=x[c * CHUNK : (c + 1) * CHUNK, :].rearrange("(t p) f -> p t f", p=P),
-            )
+            for t in range(ROW_TILES):
+                first_row = c * CHUNK + t * P
+                nc.sync.dma_start(out=prep["x"][:, t, :], in_=x[first_row : first_row + P, :])
 
         def row_statistics():
             stats = small.tile([P, ROW_TILES, 6], F32)
@@ -118,6 +116,16 @@ def tile_kanlinear_pa_t_kernel(
             )
             prep["z"] = rows_pool.tile([P, ROW_TILES, SLOTS, P], F32, name="z", bufs=1)
 
+        def first_normalise(t):
+            nc.vector.tensor_scalar(
+                out=prep["z"][:, t, :, :],
+                in0=prep["x"][:, t, :].rearrange("p (q s) -> p s q", s=SLOTS),
+                scalar1=prep["mean_var"][:, t, 0:1],
+                scalar2=prep["rstd"][:, t : t + 1],
+                op0=ALU.subtract,
+                op1=ALU.mult,
+            )
+
         def normalise(t):
             nc.scalar.activation(
                 out=prep["z"][:, t, :, :],
@@ -142,40 +150,45 @@ def tile_kanlinear_pa_t_kernel(
         def copy_to_psum(v):
             v_psum = v_pool.tile([P, CHUNK], F32)
             nc.tensor.matmul(v_psum[:], lhsT=identity[:], rhs=v, start=True, stop=True)
-            return v_psum
+            return v_psum[:]
 
-        def regroup_relu(planes, on_vector):
-            grouped = operand_pool.tile([P, CHUNK, PACK], BF16, align_bytes=64)
-            target = grouped[:].rearrange("p (b i) t -> p b t i", i=RUN)
-            source = planes.rearrange("p t (b i) -> p b t i", i=RUN)
+        def regroup_relu(grouped, planes, on_vector, first, last):
+            target = grouped[:, first:last, :].rearrange("p (b i) t -> p b t i", i=RUN)
+            source = planes[:, :, first:last].rearrange("p t (b i) -> p b t i", i=RUN)
             if on_vector:
                 nc.vector.tensor_scalar_max(out=target, in0=source, scalar1=0.0)
             else:
                 nc.scalar.activation(out=target, in_=source, func=FUNC.Relu)
-            return grouped
 
-        def quantise(grouped):
-            codes = operand_pool.tile([P, CHUNK], U32, align_bytes=64)
-            scales = operand_pool.tile([P, CHUNK], U8, align_bytes=64)
+        def new_grouped():
+            return operand_pool.tile([P, CHUNK, PACK], BF16, name="grouped", align_bytes=64)
+
+        def multiply(acc, grouped, e, first, last):
+            rows = last - first
+            codes = operand_pool.tile([P, rows], U32, align_bytes=64)
+            scales = operand_pool.tile([P, rows], U8, align_bytes=64)
             nc.vector.quantize_mx(
                 out=codes[:].bitcast(FP8X4),
                 scales=scales[:],
-                in_=grouped[:].rearrange("p r t -> p (r t)"),
+                in_=grouped[:, first:last, :].rearrange("p r t -> p (r t)"),
             )
-            return codes, scales
-
-        def multiply(acc, operand, weights, start, stop):
-            codes, scales = operand
-            for t in range(ROW_TILES):
+            if e == WORDS:
+                weights = [(base_words[:], weight_scales[:, SHARES, :])]
+            else:
+                weights = [
+                    (spline_words[:, e, share, :], weight_scales[:, share, :])
+                    for share in range(SHARES)
+                ]
+            for t in range(rows // P):
                 for n, (words, scale_plane) in enumerate(weights):
                     nc.tensor.matmul_mx(
-                        out=acc[t][:],
+                        out=acc[first // P + t][:],
                         lhsT=codes[:, t * P : (t + 1) * P].bitcast(FP8X4),
                         lhsT_scale=scales[:, t * P : (t + 1) * P],
                         rhs=words.bitcast(FP8X4),
                         rhs_scale=scale_plane,
-                        start=start and n == 0,
-                        stop=stop and n == len(weights) - 1,
+                        start=e == WORDS,
+                        stop=e == WORDS - 1 and n == SHARES - 1,
                     )
 
         def store_results(c, acc):
@@ -185,13 +198,13 @@ def tile_kanlinear_pa_t_kernel(
                 first_row = c * CHUNK + t * P
                 nc.sync.dma_start(out=out[first_row : first_row + P, :], in_=result[:])
 
+        knot_bf = keep.tile([P, SLOTS, KNOTS], BF16)
+        nc.sync.dma_start(out=knot_bf[:], in_=grid.rearrange("o (p s) k -> (o p) s k", s=SLOTS))
         load_rows(0)
         gamma_bf = keep.tile([P, SLOTS], BF16)
         beta_bf = keep.tile([P, SLOTS], BF16)
-        knot_bf = keep.tile([P, SLOTS, KNOTS], BF16)
         nc.sync.dma_start(out=gamma_bf[:], in_=ln_gamma.rearrange("(p s) -> p s", s=SLOTS))
         nc.sync.dma_start(out=beta_bf[:], in_=ln_beta.rearrange("(p s) -> p s", s=SLOTS))
-        nc.sync.dma_start(out=knot_bf[:], in_=grid.rearrange("o (p s) k -> (o p) s k", s=SLOTS))
         identity = keep.tile([P, P], F32)
         masks.make_identity(nc, identity[:])
         one = keep.tile([P, 1], F32)
@@ -203,24 +216,10 @@ def tile_kanlinear_pa_t_kernel(
         for e in range(WORDS):
             nc.gpsimd.memset(spline_words[:, e, :, :].bitcast(F32), 0.0)
 
-        gamma = keep.tile([P, SLOTS], F32)
-        beta = keep.tile([P, SLOTS], F32)
-        nc.vector.tensor_copy(out=gamma[:], in_=gamma_bf[:])
-        nc.vector.tensor_copy(out=beta[:], in_=beta_bf[:])
-        row_statistics()
-        row_std()
-        row_rstd()
-        for t in range(ROW_TILES):
-            normalise(t)
-        xn = {0: xn_pool.tile([P, SLOTS, CHUNK], F32, name="xn_tile")}
-        for s in range(SLOTS):
-            bring_xn(xn[0], s)
-        load_rows(1)
-
         knot = keep.tile([P, SLOTS, KNOTS], F32)
         nc.vector.tensor_copy(out=knot[:], in_=knot_bf[:])
         neg_knot = keep.tile([P, SLOTS, KNOTS], F32)
-        nc.vector.tensor_scalar_mul(out=neg_knot[:], in0=knot[:], scalar1=-1.0)
+        nc.scalar.activation(out=neg_knot[:], in_=knot_bf[:], func=FUNC.Identity, scale=-1.0)
         span = {}
         for d in range(1, 5):
             span[d] = keep.tile([P, SLOTS, KNOTS - d], F32, name="span%d" % d)
@@ -231,25 +230,21 @@ def tile_kanlinear_pa_t_kernel(
         def spans(d, first):
             return span[d][:, :, first : first + BASES]
 
-        c0 = product(nc, keep, "c0", [spans(1, 0), spans(2, 0), spans(3, 0)])
-        nc.vector.reciprocal(out=c0[:], in_=c0[:])
-        c1 = product(nc, keep, "c1", [spans(1, 0), spans(1, 1), spans(2, 1), spans(3, 1)])
-        nc.vector.reciprocal(out=c1[:], in_=c1[:])
-        nc.vector.tensor_mul(out=c1[:], in0=c1[:], in1=spans(4, 0))
-        neg_c4 = product(nc, keep, "neg_c4", [spans(3, 1), spans(2, 2), spans(1, 3)])
-        nc.vector.reciprocal(out=neg_c4[:], in_=neg_c4[:])
-        nc.vector.tensor_scalar_mul(out=neg_c4[:], in0=neg_c4[:], scalar1=-1.0)
-        neg_c3 = product(nc, keep, "neg_c3", [spans(3, 0), spans(2, 1), spans(1, 2), spans(1, 3)])
-        nc.vector.reciprocal(out=neg_c3[:], in_=neg_c3[:])
-        nc.vector.scalar_tensor_tensor(
-            out=neg_c3[:], in0=neg_c3[:], scalar=-1.0, in1=spans(4, 0), op0=ALU.mult, op1=ALU.mult
-        )
+        coef = keep.tile([P, 4, SLOTS, BASES], F32)
+        c0, c1, c3, c4 = [coef[:, n, :, :] for n in range(4)]
+        product(nc, c0, [spans(1, 0), spans(2, 0), spans(3, 0)])
+        product(nc, c1, [spans(1, 0), spans(1, 1), spans(2, 1), spans(3, 1)])
+        product(nc, c3, [spans(3, 0), spans(2, 1), spans(1, 2), spans(1, 3)])
+        product(nc, c4, [spans(3, 1), spans(2, 2), spans(1, 3)])
+        nc.vector.reciprocal(out=coef[:], in_=coef[:])
+        nc.vector.tensor_mul(out=c1, in0=c1, in1=spans(4, 0))
+        nc.vector.tensor_mul(out=c3, in0=c3, in1=spans(4, 0))
 
         scale = keep.tile([P, SLOTS, KNOTS], F32)
         nc.vector.tensor_copy(out=scale[:, :, 0:6:2], in_=c0[:, :, 0:6:2])
         nc.vector.tensor_copy(out=scale[:, :, 1:6:2], in_=c1[:, :, 0:6:2])
-        nc.vector.tensor_scalar_mul(out=scale[:, :, 6:10:2], in0=neg_c3[:, :, 3:6:2], scalar1=-1.0)
-        nc.vector.tensor_scalar_mul(out=scale[:, :, 7:10:2], in0=neg_c4[:, :, 3:6:2], scalar1=-1.0)
+        nc.vector.tensor_copy(out=scale[:, :, 6:10:2], in_=c3[:, :, 3:6:2])
+        nc.vector.tensor_copy(out=scale[:, :, 7:10:2], in_=c4[:, :, 3:6:2])
         rough_root = keep.tile([P, SLOTS, KNOTS], F32)
         nc.scalar.activation(out=rough_root[:], in_=scale[:], func=FUNC.Sqrt)
         root = keep.tile([P, SLOTS, KNOTS], F32)
@@ -259,13 +254,37 @@ def tile_kanlinear_pa_t_kernel(
         nc.vector.tensor_scalar_mul(out=root[:], in0=root[:], scalar1=0.5)
         neg_root_knot = keep.tile([P, SLOTS, KNOTS], F32)
         nc.vector.tensor_mul(out=neg_root_knot[:], in0=root[:], in1=neg_knot[:])
+
+        gamma = keep.tile([P, SLOTS], F32)
+        beta = keep.tile([P, SLOTS], F32)
+        nc.scalar.copy(out=gamma[:], in_=gamma_bf[:])
+        nc.scalar.copy(out=beta[:], in_=beta_bf[:])
+        row_statistics()
+        row_std()
+        row_rstd()
+        for t in range(ROW_TILES):
+            first_normalise(t)
+        xn = {0: xn_pool.tile([P, SLOTS, CHUNK], F32, name="xn_tile")}
+        for s in range(SLOTS):
+            bring_xn(xn[0], s)
+        load_rows(1)
+
         unscale = keep.tile([P, SLOTS, KNOTS], F32)
         nc.vector.tensor_mul(out=unscale[:], in0=root[:], in1=root[:])
         nc.vector.reciprocal(out=unscale[:], in_=unscale[:])
-        nc.vector.tensor_mul(out=c0[:], in0=c0[:], in1=unscale[:, :, 0:6])
-        nc.vector.tensor_mul(out=c1[:], in0=c1[:], in1=unscale[:, :, 1:7])
-        nc.vector.tensor_mul(out=neg_c3[:], in0=neg_c3[:], in1=unscale[:, :, 3:9])
-        nc.vector.tensor_mul(out=neg_c4[:], in0=neg_c4[:], in1=unscale[:, :, 4:10])
+        nc.vector.tensor_mul(out=c0, in0=c0, in1=unscale[:, :, 0:6])
+        nc.vector.tensor_mul(out=c1, in0=c1, in1=unscale[:, :, 1:7])
+        neg_c3 = keep.tile([P, SLOTS, BASES], F32)
+        neg_c4 = keep.tile([P, SLOTS, BASES], F32)
+        for negative, positive, first in ((neg_c3, c3, 3), (neg_c4, c4, 4)):
+            nc.vector.scalar_tensor_tensor(
+                out=negative[:],
+                in0=positive,
+                scalar=-1.0,
+                in1=unscale[:, :, first : first + BASES],
+                op0=ALU.mult,
+                op1=ALU.mult,
+            )
 
         bias_bf = keep.tile([P, UNITS], BF16)
         nc.sync.dma_start(out=bias_bf[:], in_=base_bias.partition_broadcast(P))
@@ -310,45 +329,49 @@ def tile_kanlinear_pa_t_kernel(
                     )
 
         planes = keep.tile([P, SLOTS * BASES, CHUNK], BF16)
-        acc = {}
-        v_next = copy_to_psum(xn[0][:, 0, :])
-        for r in range(ROUNDS + 2):
-            chunk, s = divmod(r, SLOTS)
-            computing = r < ROUNDS
-            preparing = computing and chunk + 1 < CHUNKS
 
-            if computing:
-                v = xn[chunk][:, s, :]
-                v_psum = v_next
-                square = work.tile([P, KNOTS, CHUNK], F32, bufs=2)
-                for i in GPSIMD_KNOTS + VECTOR_KNOTS:
-                    nc.scalar.activation(
-                        out=square[:, i, :],
-                        in_=v,
-                        func=FUNC.Square,
-                        bias=neg_root_knot[:, s, i : i + 1],
-                        scale=root[:, s, i : i + 1],
-                    )
-                cube = work.tile([P, KNOTS, CHUNK], F32)
-                for i in GPSIMD_KNOTS:
-                    nc.gpsimd.tensor_scalar(
-                        out=cube[:, i, :],
-                        in0=v,
-                        scalar1=1.0,
-                        scalar2=neg_knot[:, s, i : i + 1],
-                        op0=ALU.mult,
-                        op1=ALU.add,
-                    )
-                    nc.gpsimd.tensor_mul(out=cube[:, i, :], in0=cube[:, i, :], in1=square[:, i, :])
-                for i in VECTOR_KNOTS:
-                    nc.vector.scalar_tensor_tensor(
-                        out=cube[:, i, :],
-                        in0=v_psum[:],
-                        scalar=knot[:, s, i : i + 1],
-                        in1=square[:, i, :],
-                        op0=ALU.subtract,
-                        op1=ALU.mult,
-                    )
+        def word_planes(e):
+            return planes[:, PACK * e : PACK * (e + 1), :]
+
+        acc = {}
+        v_next = xn[0][:, 0, :]
+        for r in range(ROUNDS):
+            chunk, s = divmod(r, SLOTS)
+            preparing = chunk + 1 < CHUNKS
+            last_round = r == ROUNDS - 1
+
+            v = xn[chunk][:, s, :]
+            v_psum = v_next
+            square = work.tile([P, KNOTS, CHUNK], F32, bufs=2)
+            for i in SQUARE_ORDER:
+                nc.scalar.activation(
+                    out=square[:, i, :],
+                    in_=v,
+                    func=FUNC.Square,
+                    bias=neg_root_knot[:, s, i : i + 1],
+                    scale=root[:, s, i : i + 1],
+                )
+            cube = work.tile([P, KNOTS, CHUNK], F32)
+            shifted = work.tile([P, len(GPSIMD_KNOTS), CHUNK], F32, tag="rise")
+            for n, i in enumerate(GPSIMD_KNOTS):
+                nc.gpsimd.tensor_scalar(
+                    out=shifted[:, n, :],
+                    in0=v,
+                    scalar1=1.0,
+                    scalar2=neg_knot[:, s, i : i + 1],
+                    op0=ALU.mult,
+                    op1=ALU.add,
+                )
+                nc.gpsimd.tensor_mul(out=cube[:, i, :], in0=shifted[:, n, :], in1=square[:, i, :])
+            for i in VECTOR_KNOTS:
+                nc.vector.scalar_tensor_tensor(
+                    out=cube[:, i, :],
+                    in0=v_psum,
+                    scalar=knot[:, s, i : i + 1],
+                    in1=square[:, i, :],
+                    op0=ALU.subtract,
+                    op1=ALU.mult,
+                )
 
             if preparing and s == 0:
                 row_statistics()
@@ -368,75 +391,73 @@ def tile_kanlinear_pa_t_kernel(
                 store_results(chunk - 1, acc[chunk - 1])
 
             finished = []
-            if computing and s == 1:
-                finished.append((regroup_relu(xn[chunk][:], False), chunk, WORDS))
-            if 1 <= r <= ROUNDS:
+            if s == 1:
+                finished.append((xn[chunk][:], chunk, WORDS))
+            if r >= 1:
                 last_chunk, last_s = divmod(r - 1, SLOTS)
                 for e in range(BASES * last_s // PACK, BASES * (last_s + 1) // PACK):
-                    word_planes = planes[:, PACK * e : PACK * (e + 1), :]
-                    on_vector = e == WORDS - 1 and not computing
-                    finished.append((regroup_relu(word_planes, on_vector), last_chunk, e))
+                    finished.append((word_planes(e), last_chunk, e))
+            regrouped = []
+            for source, c, e in finished:
+                grouped = new_grouped()
+                regroup_relu(grouped, source, False, 0, CHUNK)
+                regrouped.append((grouped, c, e))
             if preparing and s == 3:
                 bring_xn(xn[chunk + 1], 2)
                 bring_xn(xn[chunk + 1], 3)
-            if r + 1 < ROUNDS:
+            if not last_round:
                 next_chunk, next_s = divmod(r + 1, SLOTS)
                 v_next = copy_to_psum(xn[next_chunk][:, next_s, :])
-            for grouped, c, e in finished:
-                operand = quantise(grouped)
+            for grouped, c, e in regrouped:
                 if e == WORDS:
                     acc[c] = [
                         acc_pool.tile([P, UNITS], F32, name="acc%d" % t, tag="acc")
                         for t in range(ROW_TILES)
                     ]
-                    multiply(
-                        acc[c], operand, [(base_words[:], weight_scales[:, SHARES, :])], True, False
-                    )
-                else:
-                    shares = [
-                        (spline_words[:, e, share, :], weight_scales[:, share, :])
-                        for share in range(SHARES)
-                    ]
-                    multiply(acc[c], operand, shares, False, e == WORDS - 1)
+                multiply(acc[c], grouped, e, 0, CHUNK)
 
-            if computing:
-                rise_inner = work.tile([P, BASES, CHUNK], F32)
-                fall_inner = work.tile([P, BASES, CHUNK], F32)
-                for i in VECTOR_KNOTS:
-                    if i - 1 in SINGLE_RISE:
-                        nc.scalar.activation(
-                            out=rise_inner[:, i - 1, :],
-                            in_=cube[:, i, :],
-                            func=FUNC.Relu,
-                            scale=c1[:, s, i - 1 : i],
-                        )
-                    if i - 3 in SINGLE_FALL:
-                        nc.scalar.activation(
-                            out=fall_inner[:, i - 3, :],
-                            in_=cube[:, i, :],
-                            func=FUNC.Relu,
-                            scale=neg_c3[:, s, i - 3 : i - 2],
-                        )
-                rise = work.tile([P, BASES, CHUNK], BF16)
-                fall = work.tile([P, BASES, CHUNK], BF16)
-                for j in SINGLE_RISE:
-                    nc.vector.scalar_tensor_tensor(
-                        out=rise[:, j, :],
-                        in0=cube[:, j, :],
-                        scalar=c0[:, s, j : j + 1],
-                        in1=rise_inner[:, j, :],
-                        op0=ALU.mult,
-                        op1=ALU.subtract,
+            rise_inner = work.tile([P, BASES, CHUNK], F32)
+            fall_inner = work.tile([P, BASES, CHUNK], F32)
+            for i in VECTOR_KNOTS:
+                if i - 1 in SINGLE_RISE:
+                    nc.scalar.activation(
+                        out=rise_inner[:, i - 1, :],
+                        in_=cube[:, i, :],
+                        func=FUNC.Relu,
+                        scale=c1[:, s, i - 1 : i],
                     )
-                for j in SINGLE_FALL:
-                    nc.vector.scalar_tensor_tensor(
-                        out=fall[:, j, :],
-                        in0=cube[:, j + 4, :],
-                        scalar=neg_c4[:, s, j : j + 1],
-                        in1=fall_inner[:, j, :],
-                        op0=ALU.mult,
-                        op1=ALU.subtract,
+                if i - 3 in SINGLE_FALL:
+                    nc.scalar.activation(
+                        out=fall_inner[:, i - 3, :],
+                        in_=cube[:, i, :],
+                        func=FUNC.Relu,
+                        scale=neg_c3[:, s, i - 3 : i - 2],
                     )
+
+            rise = work.tile([P, BASES, CHUNK], BF16, tag="rise")
+            fall = work.tile([P, BASES, CHUNK], BF16)
+
+            def single_rise(j):
+                nc.vector.scalar_tensor_tensor(
+                    out=rise[:, j, :],
+                    in0=cube[:, j, :],
+                    scalar=c0[:, s, j : j + 1],
+                    in1=rise_inner[:, j, :],
+                    op0=ALU.mult,
+                    op1=ALU.subtract,
+                )
+
+            def single_fall(j):
+                nc.vector.scalar_tensor_tensor(
+                    out=fall[:, j, :],
+                    in0=cube[:, j + 4, :],
+                    scalar=neg_c4[:, s, j : j + 1],
+                    in1=fall_inner[:, j, :],
+                    op0=ALU.mult,
+                    op1=ALU.subtract,
+                )
+
+            def matched_rises():
                 nc.vector.scalar_tensor_tensor(
                     out=rise[:, 0:6:2, :],
                     in0=cube[:, 1:6:2, :],
@@ -446,6 +467,8 @@ def tile_kanlinear_pa_t_kernel(
                     op1=ALU.subtract,
                     reverse1=True,
                 )
+
+            def matched_falls():
                 nc.vector.scalar_tensor_tensor(
                     out=fall[:, 3:6:2, :],
                     in0=cube[:, 6:10:2, :],
@@ -454,8 +477,44 @@ def tile_kanlinear_pa_t_kernel(
                     op0=ALU.min,
                     op1=ALU.subtract,
                 )
+
+            def maximum(first, last):
                 nc.vector.tensor_max(
-                    out=planes[:, BASES * s : BASES * (s + 1), :], in0=rise[:], in1=fall[:]
+                    out=planes[:, BASES * s + first : BASES * s + last, :],
+                    in0=rise[:, first:last, :],
+                    in1=fall[:, first:last, :],
                 )
+
+            if not last_round:
+                for j in SINGLE_RISE:
+                    single_rise(j)
+                for j in SINGLE_FALL:
+                    single_fall(j)
+                matched_rises()
+                matched_falls()
+                maximum(0, BASES)
+            else:
+                single_rise(1)
+                single_fall(0)
+                single_fall(1)
+                matched_rises()
+                maximum(0, 2)
+                grouped = new_grouped()
+                regroup_relu(grouped, word_planes(WORDS - 2), False, 0, CHUNK)
+                single_rise(3)
+                single_rise(5)
+                single_fall(2)
+                single_fall(4)
+                multiply(acc[chunk], grouped, WORDS - 2, 0, CHUNK)
+                matched_falls()
+                maximum(2, BASES)
             if preparing and s == 0:
                 row_std()
+
+        half = CHUNK // 2
+        grouped = new_grouped()
+        regroup_relu(grouped, word_planes(WORDS - 1), True, 0, half)
+        regroup_relu(grouped, word_planes(WORDS - 1), False, half, CHUNK)
+        multiply(acc[CHUNKS - 1], grouped, WORDS - 1, 0, half)
+        multiply(acc[CHUNKS - 1], grouped, WORDS - 1, half, CHUNK)
+        store_results(CHUNKS - 1, acc[CHUNKS - 1])

@@ -84,6 +84,7 @@ def tile_kanlinear_pa_t_kernel(
             prep["mean_var"] = small.tile([P, ROW_TILES, 2], F32, name="mean_var")
             for t in range(ROW_TILES):
                 nc.vector.bn_stats(out=stats[:, t, :], in_=prep["x"][:, t, :])
+            for t in range(ROW_TILES):
                 nc.vector.bn_aggr(out=prep["mean_var"][:, t, :], in_=stats[:, t, :])
             prep["var_eps"] = small.tile([P, ROW_TILES], F32, name="var_eps")
             nc.vector.tensor_scalar_add(
@@ -98,13 +99,19 @@ def tile_kanlinear_pa_t_kernel(
             rough = small.tile([P, ROW_TILES], F32)
             nc.vector.reciprocal(out=rough[:], in_=prep["std"][:])
             step = small.tile([P, ROW_TILES], F32)
-            nc.vector.tensor_mul(out=step[:], in0=rough[:], in1=rough[:])
-            nc.vector.tensor_mul(out=step[:], in0=step[:], in1=prep["var_eps"][:])
-            nc.vector.tensor_scalar(
-                out=step[:], in0=step[:], scalar1=-0.5, scalar2=1.5, op0=ALU.mult, op1=ALU.add
+            nc.vector.scalar_tensor_tensor(
+                out=step[:], in0=rough[:], scalar=-0.5, in1=rough[:], op0=ALU.mult, op1=ALU.mult
             )
+            nc.vector.tensor_mul(out=step[:], in0=step[:], in1=prep["var_eps"][:])
             prep["rstd"] = small.tile([P, ROW_TILES], F32, name="rstd")
-            nc.vector.tensor_mul(out=prep["rstd"][:], in0=rough[:], in1=step[:])
+            nc.vector.scalar_tensor_tensor(
+                out=prep["rstd"][:],
+                in0=step[:],
+                scalar=1.5,
+                in1=rough[:],
+                op0=ALU.add,
+                op1=ALU.mult,
+            )
             prep["shift"] = small.tile([P, ROW_TILES], F32, name="shift")
             nc.vector.scalar_tensor_tensor(
                 out=prep["shift"][:],
@@ -478,11 +485,12 @@ def tile_kanlinear_pa_t_kernel(
                     op1=ALU.subtract,
                 )
 
-            def maximum(first, last):
+            def maximum(first, last, step=1):
+                bases = slice(first, last, step)
                 nc.vector.tensor_max(
-                    out=planes[:, BASES * s + first : BASES * s + last, :],
-                    in0=rise[:, first:last, :],
-                    in1=fall[:, first:last, :],
+                    out=planes[:, BASES * s + first : BASES * s + last : step, :],
+                    in0=rise[:, bases, :],
+                    in1=fall[:, bases, :],
                 )
 
             if not last_round:
@@ -490,9 +498,11 @@ def tile_kanlinear_pa_t_kernel(
                     single_rise(j)
                 for j in SINGLE_FALL:
                     single_fall(j)
-                matched_rises()
                 matched_falls()
-                maximum(0, BASES)
+                matched_rises()
+                maximum(3, BASES, 2)
+                maximum(0, 3)
+                maximum(4, 5)
             else:
                 single_rise(1)
                 single_fall(0)

@@ -79,13 +79,40 @@ def tile_kanlinear_pa_t_kernel(
                 first_row = c * CHUNK + t * P
                 nc.sync.dma_start(out=prep["x"][:, t, :], in_=x[first_row : first_row + P, :])
 
-        def row_statistics():
+        def row_sum(t, func, bias):
+            unused = small.tile([P, FEATURES], BF16)
+            total = small.tile([P, 1], F32)
+            nc.scalar.activation(
+                out=unused[:],
+                in_=prep["x"][:, t, :],
+                func=func,
+                bias=bias,
+                scale=1.0,
+                accum_out=total[:],
+            )
+            return total
+
+        def row_statistics(by_scalar):
             stats = small.tile([P, ROW_TILES, 6], F32)
             prep["mean_var"] = small.tile([P, ROW_TILES, 2], F32, name="mean_var")
-            for t in range(ROW_TILES):
+            by_vector = ROW_TILES - by_scalar
+            for t in range(by_vector):
                 nc.vector.bn_stats(out=stats[:, t, :], in_=prep["x"][:, t, :])
-            for t in range(ROW_TILES):
+            for t in range(by_vector):
                 nc.vector.bn_aggr(out=prep["mean_var"][:, t, :], in_=stats[:, t, :])
+            for t in range(by_vector, ROW_TILES):
+                total = row_sum(t, FUNC.Identity, 0.0)
+                neg_mean = small.tile([P, 1], F32)
+                nc.vector.tensor_scalar_mul(
+                    out=neg_mean[:], in0=total[:], scalar1=-1.0 / FEATURES
+                )
+                total = row_sum(t, FUNC.Square, neg_mean[:])
+                nc.vector.tensor_scalar_mul(
+                    out=prep["mean_var"][:, t, 0:1], in0=neg_mean[:], scalar1=-1.0
+                )
+                nc.vector.tensor_scalar_mul(
+                    out=prep["mean_var"][:, t, 1:2], in0=total[:], scalar1=1.0 / FEATURES
+                )
             prep["var_eps"] = small.tile([P, ROW_TILES], F32, name="var_eps")
             nc.vector.tensor_scalar_add(
                 out=prep["var_eps"][:], in0=prep["mean_var"][:, :, 1], scalar1=LN_EPS
@@ -266,7 +293,7 @@ def tile_kanlinear_pa_t_kernel(
         beta = keep.tile([P, SLOTS], F32)
         nc.scalar.copy(out=gamma[:], in_=gamma_bf[:])
         nc.scalar.copy(out=beta[:], in_=beta_bf[:])
-        row_statistics()
+        row_statistics(0)
         row_std()
         row_rstd()
         for t in range(ROW_TILES):
@@ -381,7 +408,7 @@ def tile_kanlinear_pa_t_kernel(
                 )
 
             if preparing and s == 0:
-                row_statistics()
+                row_statistics(1)
             if preparing and s == 1:
                 row_rstd()
                 normalise(0)

from contextlib import ExitStack

import concourse.masks as masks
import concourse.mybir as mybir

F32 = mybir.dt.float32
BF16 = mybir.dt.bfloat16
I32 = mybir.dt.int32
U32 = mybir.dt.uint32
U8 = mybir.dt.uint8
FP8X4 = mybir.dt.float8_e4m3fn_x4
ALU = mybir.AluOpType
FUNC = mybir.ActivationFunctionType

ROWS = 4096
FEATURES = 512
UNITS = 256
KNOTS = 10
BASES = 6
LN_EPS = 0.001

P = 128
PACK = 4
SLOTS = FEATURES // P
WORDS = SLOTS * BASES // PACK
SHARES = 6
BLOCK_PARTITIONS = 8
CHUNK = 512
ROW_TILES = CHUNK // P
CHUNKS = ROWS // CHUNK
ROUNDS = CHUNKS * SLOTS
RUN = 4
GPSIMD_KNOTS = (0, 9)
VECTOR_KNOTS = (2, 3, 4, 5, 6, 7, 1, 8)
SQUARE_ORDER = (2, 3, 0, 4, 9, 5, 6, 7, 1, 8)
SINGLE_RISE = (1, 3, 5)
SINGLE_FALL = (0, 1, 2, 4)

FLOPS = 2 * ROWS * (FEATURES + FEATURES * BASES) * UNITS


def product(nc, result, factors):
    nc.vector.tensor_mul(out=result, in0=factors[0], in1=factors[1])
    for factor in factors[2:]:
        nc.vector.tensor_mul(out=result, in0=result, in1=factor)


def tile_kanlinear_pa_t_kernel(
    tc,
    x,
    ln_gamma,
    ln_beta,
    base_weight_words,
    base_weight_scales,
    base_bias,
    spline_weight_words,
    spline_weight_scales,
    grid,
    out,
):
    nc = tc.nc
    with ExitStack() as stack:
        keep = stack.enter_context(tc.tile_pool(name="keep", bufs=1))
        rows_pool = stack.enter_context(tc.tile_pool(name="rows", bufs=2))
        small = stack.enter_context(tc.tile_pool(name="small", bufs=2))
        xn_pool = stack.enter_context(tc.tile_pool(name="xn", bufs=2))
        work = stack.enter_context(tc.tile_pool(name="work", bufs=1))
        operand_pool = stack.enter_context(tc.tile_pool(name="operands", bufs=4))
        result_pool = stack.enter_context(tc.tile_pool(name="results", bufs=4))
        transposed_pool = stack.enter_context(tc.psum_pool(name="transposed", bufs=2))
        v_pool = stack.enter_context(tc.psum_pool(name="v", bufs=2))
        acc_pool = stack.enter_context(tc.psum_pool(name="acc", bufs=ROW_TILES))

        prep = {}

        def load_rows(c):
            prep["x"] = rows_pool.tile([P, ROW_TILES, FEATURES], BF16, name="x_rows")
            for t in range(ROW_TILES):
                first_row = c * CHUNK + t * P
                nc.sync.dma_start(out=prep["x"][:, t, :], in_=x[first_row : first_row + P, :])

        def row_sum(t, func, bias):
            unused = small.tile([P, FEATURES], BF16)
            total = small.tile([P, 1], F32)
            nc.scalar.activation(
                out=unused[:],
                in_=prep["x"][:, t, :],
                func=func,
                bias=bias,
                scale=1.0,
                accum_out=total[:],
            )
            return total

        def row_statistics(by_scalar):
            stats = small.tile([P, ROW_TILES, 6], F32)
            prep["mean_var"] = small.tile([P, ROW_TILES, 2], F32, name="mean_var")
            by_vector = ROW_TILES - by_scalar
            for t in range(by_vector):
                nc.vector.bn_stats(out=stats[:, t, :], in_=prep["x"][:, t, :])
            for t in range(by_vector):
                nc.vector.bn_aggr(out=prep["mean_var"][:, t, :], in_=stats[:, t, :])
            for t in range(by_vector, ROW_TILES):
                total = row_sum(t, FUNC.Identity, 0.0)
                neg_mean = small.tile([P, 1], F32)
                nc.vector.tensor_scalar_mul(
                    out=neg_mean[:], in0=total[:], scalar1=-1.0 / FEATURES
                )
                total = row_sum(t, FUNC.Square, neg_mean[:])
                nc.vector.tensor_scalar_mul(
                    out=prep["mean_var"][:, t, 0:1], in0=neg_mean[:], scalar1=-1.0
                )
                nc.vector.tensor_scalar_mul(
                    out=prep["mean_var"][:, t, 1:2], in0=total[:], scalar1=1.0 / FEATURES
                )
            prep["var_eps"] = small.tile([P, ROW_TILES], F32, name="var_eps")
            nc.vector.tensor_scalar_add(
                out=prep["var_eps"][:], in0=prep["mean_var"][:, :, 1], scalar1=LN_EPS
            )

        def row_std():
            prep["std"] = small.tile([P, ROW_TILES], F32, name="std")
            nc.scalar.activation(out=prep["std"][:], in_=prep["var_eps"][:], func=FUNC.Sqrt)

        def row_rstd():
            rough = small.tile([P, ROW_TILES], F32)
            nc.vector.reciprocal(out=rough[:], in_=prep["std"][:])
            step = small.tile([P, ROW_TILES], F32)
            nc.vector.scalar_tensor_tensor(
                out=step[:], in0=rough[:], scalar=-0.5, in1=rough[:], op0=ALU.mult, op1=ALU.mult
            )
            nc.vector.tensor_mul(out=step[:], in0=step[:], in1=prep["var_eps"][:])
            prep["rstd"] = small.tile([P, ROW_TILES], F32, name="rstd")
            nc.vector.scalar_tensor_tensor(
                out=prep["rstd"][:],
                in0=step[:],
                scalar=1.5,
                in1=rough[:],
                op0=ALU.add,
                op1=ALU.mult,
            )
            prep["shift"] = small.tile([P, ROW_TILES], F32, name="shift")
            nc.vector.scalar_tensor_tensor(
                out=prep["shift"][:],
                in0=prep["mean_var"][:, :, 0],
                scalar=-1.0,
                in1=prep["rstd"][:],
                op0=ALU.mult,
                op1=ALU.mult,
            )
            prep["z"] = rows_pool.tile([P, ROW_TILES, SLOTS, P], F32, name="z", bufs=1)

        def first_normalise(t):
            nc.vector.tensor_scalar(
                out=prep["z"][:, t, :, :],
                in0=prep["x"][:, t, :].rearrange("p (q s) -> p s q", s=SLOTS),
                scalar1=prep["mean_var"][:, t, 0:1],
                scalar2=prep["rstd"][:, t : t + 1],
                op0=ALU.subtract,
                op1=ALU.mult,
            )

        def normalise(t):
            nc.scalar.activation(
                out=prep["z"][:, t, :, :],
                in_=prep["x"][:, t, :].rearrange("p (q s) -> p s q", s=SLOTS),
                func=FUNC.Identity,
                scale=prep["rstd"][:, t : t + 1],
                bias=prep["shift"][:, t : t + 1],
            )

        def bring_xn(xn, s):
            z_t = transposed_pool.tile([P, CHUNK], F32)
            for t in range(ROW_TILES):
                nc.tensor.transpose(z_t[:, t * P : (t + 1) * P], prep["z"][:, t, s, :], identity[:])
            nc.scalar.activation(
                out=xn[:, s, :],
                in_=z_t[:],
                func=FUNC.Identity,
                scale=gamma[:, s : s + 1],
                bias=beta[:, s : s + 1],
            )

        def copy_to_psum(v):
            v_psum = v_pool.tile([P, CHUNK], F32)
            nc.tensor.matmul(v_psum[:], lhsT=identity[:], rhs=v, start=True, stop=True)
            return v_psum[:]

        def regroup_relu(grouped, planes, on_vector, first, last):
            target = grouped[:, first:last, :].rearrange("p (b i) t -> p b t i", i=RUN)
            source = planes[:, :, first:last].rearrange("p t (b i) -> p b t i", i=RUN)
            if on_vector:
                nc.vector.tensor_scalar_max(out=target, in0=source, scalar1=0.0)
            else:
                nc.scalar.activation(out=target, in_=source, func=FUNC.Relu)

        def new_grouped():
            return operand_pool.tile([P, CHUNK, PACK], BF16, name="grouped", align_bytes=64)

        def multiply(acc, grouped, e, first, last):
            rows = last - first
            codes = operand_pool.tile([P, rows], U32, align_bytes=64)
            scales = operand_pool.tile([P, rows], U8, align_bytes=64)
            nc.vector.quantize_mx(
                out=codes[:].bitcast(FP8X4),
                scales=scales[:],
                in_=grouped[:, first:last, :].rearrange("p r t -> p (r t)"),
            )
            if e == WORDS:
                weights = [(base_words[:], weight_scales[:, SHARES, :])]
            else:
                weights = [
                    (spline_words[:, e, share, :], weight_scales[:, share, :])
                    for share in range(SHARES)
                ]
            for t in range(rows // P):
                for n, (words, scale_plane) in enumerate(weights):
                    nc.tensor.matmul_mx(
                        out=acc[first // P + t][:],
                        lhsT=codes[:, t * P : (t + 1) * P].bitcast(FP8X4),
                        lhsT_scale=scales[:, t * P : (t + 1) * P],
                        rhs=words.bitcast(FP8X4),
                        rhs_scale=scale_plane,
                        start=e == WORDS,
                        stop=e == WORDS - 1 and n == SHARES - 1,
                    )

        def store_results(c, acc):
            for t in range(ROW_TILES):
                result = result_pool.tile([P, UNITS], F32)
                nc.vector.tensor_add(out=result[:], in0=acc[t][:], in1=bias[:])
                first_row = c * CHUNK + t * P
                nc.sync.dma_start(out=out[first_row : first_row + P, :], in_=result[:])

        knot_bf = keep.tile([P, SLOTS, KNOTS], BF16)
        nc.sync.dma_start(out=knot_bf[:], in_=grid.rearrange("o (p s) k -> (o p) s k", s=SLOTS))
        load_rows(0)
        gamma_bf = keep.tile([P, SLOTS], BF16)
        beta_bf = keep.tile([P, SLOTS], BF16)
        nc.sync.dma_start(out=gamma_bf[:], in_=ln_gamma.rearrange("(p s) -> p s", s=SLOTS))
        nc.sync.dma_start(out=beta_bf[:], in_=ln_beta.rearrange("(p s) -> p s", s=SLOTS))
        identity = keep.tile([P, P], F32)
        masks.make_identity(nc, identity[:])
        one = keep.tile([P, 1], F32)
        nc.vector.memset(one[:], 1.0)
        nc.scalar.activation(out=one[:], in_=one[:], func=FUNC.Sqrt)
        weight_scales = keep.tile([P, SHARES + 1, UNITS], U8, align_bytes=64)
        nc.vector.memset(weight_scales[:].bitcast(I32), 0)
        spline_words = keep.tile([P, WORDS, SHARES, UNITS], I32, align_bytes=64)
        for e in range(WORDS):
            nc.gpsimd.memset(spline_words[:, e, :, :].bitcast(F32), 0.0)

        knot = keep.tile([P, SLOTS, KNOTS], F32)
        nc.vector.tensor_copy(out=knot[:], in_=knot_bf[:])
        neg_knot = keep.tile([P, SLOTS, KNOTS], F32)
        nc.scalar.activation(out=neg_knot[:], in_=knot_bf[:], func=FUNC.Identity, scale=-1.0)
        span = {}
        for d in range(1, 5):
            span[d] = keep.tile([P, SLOTS, KNOTS - d], F32, name="span%d" % d)
            nc.vector.tensor_sub(
                out=span[d][:], in0=knot[:, :, d:KNOTS], in1=knot[:, :, 0 : KNOTS - d]
            )

        def spans(d, first):
            return span[d][:, :, first : first + BASES]

        coef = keep.tile([P, 4, SLOTS, BASES], F32)
        c0, c1, c3, c4 = [coef[:, n, :, :] for n in range(4)]
        product(nc, c0, [spans(1, 0), spans(2, 0), spans(3, 0)])
        product(nc, c1, [spans(1, 0), spans(1, 1), spans(2, 1), spans(3, 1)])
        product(nc, c3, [spans(3, 0), spans(2, 1), spans(1, 2), spans(1, 3)])
        product(nc, c4, [spans(3, 1), spans(2, 2), spans(1, 3)])
        nc.vector.reciprocal(out=coef[:], in_=coef[:])
        nc.vector.tensor_mul(out=c1, in0=c1, in1=spans(4, 0))
        nc.vector.tensor_mul(out=c3, in0=c3, in1=spans(4, 0))

        scale = keep.tile([P, SLOTS, KNOTS], F32)
        nc.vector.tensor_copy(out=scale[:, :, 0:6:2], in_=c0[:, :, 0:6:2])
        nc.vector.tensor_copy(out=scale[:, :, 1:6:2], in_=c1[:, :, 0:6:2])
        nc.vector.tensor_copy(out=scale[:, :, 6:10:2], in_=c3[:, :, 3:6:2])
        nc.vector.tensor_copy(out=scale[:, :, 7:10:2], in_=c4[:, :, 3:6:2])
        rough_root = keep.tile([P, SLOTS, KNOTS], F32)
        nc.scalar.activation(out=rough_root[:], in_=scale[:], func=FUNC.Sqrt)
        root = keep.tile([P, SLOTS, KNOTS], F32)
        nc.vector.reciprocal(out=root[:], in_=rough_root[:])
        nc.vector.tensor_mul(out=root[:], in0=root[:], in1=scale[:])
        nc.vector.tensor_add(out=root[:], in0=root[:], in1=rough_root[:])
        nc.vector.tensor_scalar_mul(out=root[:], in0=root[:], scalar1=0.5)
        neg_root_knot = keep.tile([P, SLOTS, KNOTS], F32)
        nc.vector.tensor_mul(out=neg_root_knot[:], in0=root[:], in1=neg_knot[:])

        gamma = keep.tile([P, SLOTS], F32)
        beta = keep.tile([P, SLOTS], F32)
        nc.scalar.copy(out=gamma[:], in_=gamma_bf[:])
        nc.scalar.copy(out=beta[:], in_=beta_bf[:])
        row_statistics(0)
        row_std()
        row_rstd()
        for t in range(ROW_TILES):
            first_normalise(t)
        xn = {0: xn_pool.tile([P, SLOTS, CHUNK], F32, name="xn_tile")}
        for s in range(SLOTS):
            bring_xn(xn[0], s)
        load_rows(1)

        unscale = keep.tile([P, SLOTS, KNOTS], F32)
        nc.vector.tensor_mul(out=unscale[:], in0=root[:], in1=root[:])
        nc.vector.reciprocal(out=unscale[:], in_=unscale[:])
        nc.vector.tensor_mul(out=c0, in0=c0, in1=unscale[:, :, 0:6])
        nc.vector.tensor_mul(out=c1, in0=c1, in1=unscale[:, :, 1:7])
        neg_c3 = keep.tile([P, SLOTS, BASES], F32)
        neg_c4 = keep.tile([P, SLOTS, BASES], F32)
        for negative, positive, first in ((neg_c3, c3, 3), (neg_c4, c4, 4)):
            nc.vector.scalar_tensor_tensor(
                out=negative[:],
                in0=positive,
                scalar=-1.0,
                in1=unscale[:, :, first : first + BASES],
                op0=ALU.mult,
                op1=ALU.mult,
            )

        bias_bf = keep.tile([P, UNITS], BF16)
        nc.sync.dma_start(out=bias_bf[:], in_=base_bias.partition_broadcast(P))
        bias = keep.tile([P, UNITS], F32)
        nc.vector.tensor_copy(out=bias[:], in_=bias_bf[:])

        spline_scale_rows = (
            spline_weight_scales.rearrange("g r n -> (g r) n")
            .bitcast(I32)
            .rearrange("(a b c) n -> b a c n", a=4, b=4, c=SHARES)
        )
        base_scale_rows = (
            base_weight_scales.rearrange("g r n -> (g r) n")
            .bitcast(I32)
            .rearrange("(a b) n -> b a n", a=4)
        )
        for b in range(4):
            nc.sync.dma_start(
                out=weight_scales[b:P:32, 0:SHARES, :].bitcast(I32), in_=spline_scale_rows[b]
            )
            nc.sync.dma_start(
                out=weight_scales[b:P:32, SHARES, :].bitcast(I32), in_=base_scale_rows[b]
            )
        base_words = keep.tile([P, UNITS], I32, align_bytes=64)
        nc.sync.dma_start(
            out=base_words[:],
            in_=base_weight_words.rearrange("g p n t -> (g p) (n t)").bitcast(I32),
        )
        word_rows = (
            spline_weight_words.rearrange("g p n t -> (g p) (n t)")
            .bitcast(I32)
            .rearrange("(q i e) n -> i q e n", i=BLOCK_PARTITIONS, e=WORDS)
        )
        for i in range(BLOCK_PARTITIONS):
            for c in range(SHARES):
                members = [e for e in range(WORDS) if (WORDS * i + e) // BLOCK_PARTITIONS == c]
                if members:
                    first, last = members[0], members[-1] + 1
                    nc.sync.dma_start(
                        out=spline_words[i:P:BLOCK_PARTITIONS, first:last, c, :],
                        in_=word_rows[i][:, first:last, :],
                    )

        planes = keep.tile([P, SLOTS * BASES, CHUNK], BF16)

        def word_planes(e):
            return planes[:, PACK * e : PACK * (e + 1), :]

        acc = {}
        v_next = xn[0][:, 0, :]
        for r in range(ROUNDS):
            chunk, s = divmod(r, SLOTS)
            preparing = chunk + 1 < CHUNKS
            last_round = r == ROUNDS - 1

            v = xn[chunk][:, s, :]
            v_psum = v_next
            square = work.tile([P, KNOTS, CHUNK], F32, bufs=2)
            for i in SQUARE_ORDER:
                nc.scalar.activation(
                    out=square[:, i, :],
                    in_=v,
                    func=FUNC.Square,
                    bias=neg_root_knot[:, s, i : i + 1],
                    scale=root[:, s, i : i + 1],
                )
            cube = work.tile([P, KNOTS, CHUNK], F32)
            shifted = work.tile([P, len(GPSIMD_KNOTS), CHUNK], F32, tag="rise")
            for n, i in enumerate(GPSIMD_KNOTS):
                nc.gpsimd.tensor_scalar(
                    out=shifted[:, n, :],
                    in0=v,
                    scalar1=1.0,
                    scalar2=neg_knot[:, s, i : i + 1],
                    op0=ALU.mult,
                    op1=ALU.add,
                )
                nc.gpsimd.tensor_mul(out=cube[:, i, :], in0=shifted[:, n, :], in1=square[:, i, :])
            for i in VECTOR_KNOTS:
                nc.vector.scalar_tensor_tensor(
                    out=cube[:, i, :],
                    in0=v_psum,
                    scalar=knot[:, s, i : i + 1],
                    in1=square[:, i, :],
                    op0=ALU.subtract,
                    op1=ALU.mult,
                )

            if preparing and s == 0:
                row_statistics(1)
            if preparing and s == 1:
                row_rstd()
                normalise(0)
                normalise(1)
            if preparing and s == 2:
                normalise(2)
                normalise(3)
                xn[chunk + 1] = xn_pool.tile([P, SLOTS, CHUNK], F32, name="xn_tile")
                bring_xn(xn[chunk + 1], 0)
                bring_xn(xn[chunk + 1], 1)
                if chunk + 2 < CHUNKS:
                    load_rows(chunk + 2)
            if s == 1 and chunk >= 1:
                store_results(chunk - 1, acc[chunk - 1])

            finished = []
            if s == 1:
                finished.append((xn[chunk][:], chunk, WORDS))
            if r >= 1:
                last_chunk, last_s = divmod(r - 1, SLOTS)
                for e in range(BASES * last_s // PACK, BASES * (last_s + 1) // PACK):
                    finished.append((word_planes(e), last_chunk, e))
            regrouped = []
            for source, c, e in finished:
                grouped = new_grouped()
                regroup_relu(grouped, source, False, 0, CHUNK)
                regrouped.append((grouped, c, e))
            if preparing and s == 3:
                bring_xn(xn[chunk + 1], 2)
                bring_xn(xn[chunk + 1], 3)
            if not last_round:
                next_chunk, next_s = divmod(r + 1, SLOTS)
                v_next = copy_to_psum(xn[next_chunk][:, next_s, :])
            for grouped, c, e in regrouped:
                if e == WORDS:
                    acc[c] = [
                        acc_pool.tile([P, UNITS], F32, name="acc%d" % t, tag="acc")
                        for t in range(ROW_TILES)
                    ]
                multiply(acc[c], grouped, e, 0, CHUNK)

            rise_inner = work.tile([P, BASES, CHUNK], F32)
            fall_inner = work.tile([P, BASES, CHUNK], F32)
            for i in VECTOR_KNOTS:
                if i - 1 in SINGLE_RISE:
                    nc.scalar.activation(
                        out=rise_inner[:, i - 1, :],
                        in_=cube[:, i, :],
                        func=FUNC.Relu,
                        scale=c1[:, s, i - 1 : i],
                    )
                if i - 3 in SINGLE_FALL:
                    nc.scalar.activation(
                        out=fall_inner[:, i - 3, :],
                        in_=cube[:, i, :],
                        func=FUNC.Relu,
                        scale=neg_c3[:, s, i - 3 : i - 2],
                    )

            rise = work.tile([P, BASES, CHUNK], BF16, tag="rise")
            fall = work.tile([P, BASES, CHUNK], BF16)

            def single_rise(j):
                nc.vector.scalar_tensor_tensor(
                    out=rise[:, j, :],
                    in0=cube[:, j, :],
                    scalar=c0[:, s, j : j + 1],
                    in1=rise_inner[:, j, :],
                    op0=ALU.mult,
                    op1=ALU.subtract,
                )

            def single_fall(j):
                nc.vector.scalar_tensor_tensor(
                    out=fall[:, j, :],
                    in0=cube[:, j + 4, :],
                    scalar=neg_c4[:, s, j : j + 1],
                    in1=fall_inner[:, j, :],
                    op0=ALU.mult,
                    op1=ALU.subtract,
                )

            def matched_rises():
                nc.vector.scalar_tensor_tensor(
                    out=rise[:, 0:6:2, :],
                    in0=cube[:, 1:6:2, :],
                    scalar=0.0,
                    in1=cube[:, 0:6:2, :],
                    op0=ALU.max,
                    op1=ALU.subtract,
                    reverse1=True,
                )

            def matched_falls():
                nc.vector.scalar_tensor_tensor(
                    out=fall[:, 3:6:2, :],
                    in0=cube[:, 6:10:2, :],
                    scalar=0.0,
                    in1=cube[:, 7:10:2, :],
                    op0=ALU.min,
                    op1=ALU.subtract,
                )

            def maximum(first, last, step=1):
                bases = slice(first, last, step)
                nc.vector.tensor_max(
                    out=planes[:, BASES * s + first : BASES * s + last : step, :],
                    in0=rise[:, bases, :],
                    in1=fall[:, bases, :],
                )

            if not last_round:
                for j in SINGLE_RISE:
                    single_rise(j)
                for j in SINGLE_FALL:
                    single_fall(j)
                matched_falls()
                matched_rises()
                maximum(3, BASES, 2)
                maximum(0, 3)
                maximum(4, 5)
            else:
                single_rise(1)
                single_fall(0)
                single_fall(1)
                matched_rises()
                maximum(0, 2)
                grouped = new_grouped()
                regroup_relu(grouped, word_planes(WORDS - 2), False, 0, CHUNK)
                single_rise(3)
                single_rise(5)
                single_fall(2)
                single_fall(4)
                multiply(acc[chunk], grouped, WORDS - 2, 0, CHUNK)
                matched_falls()
                maximum(2, BASES)
            if preparing and s == 0:
                row_std()

        half = CHUNK // 2
        grouped = new_grouped()
        regroup_relu(grouped, word_planes(WORDS - 1), True, 0, half)
        regroup_relu(grouped, word_planes(WORDS - 1), False, half, CHUNK)
        multiply(acc[CHUNKS - 1], grouped, WORDS - 1, 0, half)
        multiply(acc[CHUNKS - 1], grouped, WORDS - 1, half, CHUNK)
        store_results(CHUNKS - 1, acc[CHUNKS - 1])
